import numpy as np
import ml_dtypes


def mxq(x, axis, fmt="e4m3"):
    dtype, down = {"e4m3": (ml_dtypes.float8_e4m3fn, 7), "e5m2": (ml_dtypes.float8_e5m2, 14)}[fmt]
    v = np.moveaxis(np.asarray(x, np.float32).astype(ml_dtypes.bfloat16).astype(np.float64), axis, -1)
    blocks = v.reshape(v.shape[:-1] + (-1, 32))
    amax = np.abs(blocks).max(-1, keepdims=True)
    byte = np.maximum(np.where(amax > 0, np.frexp(amax)[1] - 1 + 127, 0) - down, 1)
    scale = np.exp2(byte - 127.0)
    codes = (blocks / scale).astype(np.float32).astype(dtype).astype(np.float64)
    return np.moveaxis((codes * scale).reshape(v.shape), -1, axis)


WIDE = False


def mx_kscale(k):
    if not WIDE:
        return np.ones(k)
    levels = np.array([10, -10, 5, -5, 0])
    a = np.random.permutation(np.resize(levels, k // 512 * 4)).reshape(k // 512, 4)
    idx = np.arange(k)
    return np.exp2(a[idx // 512, idx % 128 // 32])


BF16 = ml_dtypes.bfloat16


def bf(x):
    return np.asarray(x, np.float32).astype(BF16)


def f64(x):
    return np.asarray(x).astype(np.float64)


N, C, O, OH, OW, KH, KW, STRIDE, PAD = 64, 512, 256, 4, 4, 3, 3, 1, 1
H, W = (OH - 1) * STRIDE + KH - 2 * PAD, (OW - 1) * STRIDE + KW - 2 * PAD
NEG_SLOPE = 0.1


def span(t, n_out, n_in):
    ok = [p for p in range(n_out) if 0 <= p * STRIDE + t - PAD < n_in]
    return ok[0], ok[-1] + 1


def setup_inputs():
    s = mx_kscale(C)
    return {"x": bf(np.random.standard_normal((N, C, H, W)) * s[None, :, None, None]),
            "weight": bf(np.random.standard_normal((1, O, C, OH, OW, KH * KW)) * np.sqrt(2.0 / (KH * KW * C)) / s[None, None, :, None, None, None]),
            "bias": bf(np.random.standard_normal((1, O, OH, OW)) * 0.3)}


def reference(x, weight, bias):
    xq = mxq(f64(x), 1, "e4m3")
    wt = f64(weight)[0]
    acc = np.zeros((N, O, OH, OW))
    for i in range(KH):
        h0, h1 = span(i, OH, H)
        a0 = h0 * STRIDE + i - PAD
        for j in range(KW):
            w0, w1 = span(j, OW, W)
            b0 = w0 * STRIDE + j - PAD
            xs = xq[:, :, a0:a0 + (h1 - h0 - 1) * STRIDE + 1:STRIDE, b0:b0 + (w1 - w0 - 1) * STRIDE + 1:STRIDE]
            wq = mxq(wt[:, :, h0:h1, w0:w1, i * KW + j], 1, "e4m3")
            p = xs.transpose(2, 3, 0, 1) @ wq.transpose(2, 3, 1, 0)
            acc[:, :, h0:h1, w0:w1] += p.transpose(2, 3, 0, 1)
    out = acc + f64(bias)
    return np.where(out >= 0, out, NEG_SLOPE * out)

@@ -1,0 +1,162 @@
+from contextlib import ExitStack
+
+import concourse.mybir as mybir
+
+FP8X4 = mybir.dt.float8_e4m3fn_x4
+BF16 = mybir.dt.bfloat16
+F32 = mybir.dt.float32
+U32 = mybir.dt.uint32
+U8 = mybir.dt.uint8
+ALU = mybir.AluOpType
+
+P = 128
+PACK = 4
+BATCH = 64
+C_IN = P * PACK
+C_OUT = 256
+SIDE = 4
+PLACES = SIDE * SIDE
+KSIDE = 3
+PAD = 1
+COLS = PLACES * KSIDE * KSIDE
+NEG_SLOPE = 0.1
+
+PIECE_O = 16
+SUB_O = 64
+WINDOW_O = 128
+PIECES = SUB_O // PIECE_O
+SUBS = C_OUT // SUB_O
+SUB_ROWS = SUB_O * PACK
+
+VALID_TAPS = 100
+FLOPS = 2 * BATCH * C_OUT * C_IN * VALID_TAPS
+
+
+def valid_taps(place):
+    return max(0, PAD - place), min(KSIDE, SIDE + PAD - place)
+
+
+def tile_locallyconnected2d_kernel(tc, x, weight, bias, out):
+    nc = tc.nc
+    places = [(h, w) for h in range(SIDE) for w in range(SIDE)]
+    with ExitStack() as ctx:
+        stage = ctx.enter_context(tc.tile_pool(name="stage", bufs=4))
+        keep = ctx.enter_context(tc.tile_pool(name="keep", bufs=1))
+        work = ctx.enter_context(tc.tile_pool(name="work", bufs=2))
+        psum = ctx.enter_context(tc.psum_pool(name="psum", bufs=4))
+
+        x_raw = stage.tile([P, BATCH, PACK * PLACES], BF16, tag="stage", align_bytes=64)
+        nc.sync.dma_start(out=x_raw[:], in_=x.rearrange("n (p q) a b -> p n (q a b)", q=PACK))
+        x_grouped = stage.tile([P, PLACES, 2, BATCH, PACK], BF16, tag="stage", align_bytes=64)
+        x_by_place = x_raw[:].rearrange("p n (q s) -> p s n q", q=PACK)
+        nc.vector.tensor_copy(out=x_grouped[:, :, 0, :, :], in_=x_by_place)
+        nc.scalar.copy(out=x_grouped[:, :, 1, :, :], in_=x_by_place)
+        x_codes = keep.tile([P, PLACES, 2 * BATCH], U32, align_bytes=64)
+        x_scales = keep.tile([P, PLACES, 2 * BATCH], U8, align_bytes=64)
+        for lo in range(0, PLACES, PLACES // 2):
+            some = slice(lo, lo + PLACES // 2)
+            nc.vector.quantize_mx(
+                out=x_codes[:, some, :].rearrange("p s m -> p (s m)").bitcast(FP8X4),
+                scales=x_scales[:, some, :].rearrange("p s m -> p (s m)"),
+                in_=x_grouped[:, some, :, :, :].rearrange("p s d n q -> p (s d n q)"),
+            )
+
+        bias_all = keep.tile([P, C_OUT, PLACES], BF16)
+        nc.sync.dma_start(
+            out=bias_all[:].rearrange("p o s -> p (o s)"),
+            in_=bias.rearrange("u o a b -> (u o a b)").partition_broadcast(P),
+        )
+
+        grouped = {}
+        w_codes = {}
+        w_scales = {}
+        for h, w in places:
+            i0, i1 = valid_taps(h)
+            j0, j1 = valid_taps(w)
+            grouped[(h, w)] = keep.tile(
+                [P, i1 - i0, j1 - j0, SUB_ROWS], BF16, name="grouped_%d%d" % (h, w), align_bytes=64
+            )
+            w_codes[(h, w)] = keep.tile(
+                [P, i1 - i0, j1 - j0, WINDOW_O], U32, name="w_codes_%d%d" % (h, w), align_bytes=64
+            )
+            w_scales[(h, w)] = keep.tile(
+                [P, i1 - i0, j1 - j0, WINDOW_O], U8, name="w_scales_%d%d" % (h, w), align_bytes=64
+            )
+
+        w_rows = weight.rearrange("u o (p q) h w t -> p (u o) (q h w t)", q=PACK)
+        out_rows = out.rearrange("n o a b -> n o (a b)")
+
+        for sub in range(SUBS):
+            for piece in range(PIECES):
+                o0 = sub * SUB_O + piece * PIECE_O
+                raw = stage.tile([P, PIECE_O, PACK * COLS], BF16, tag="stage", align_bytes=64)
+                nc.sync.dma_start(out=raw[:], in_=w_rows[:, o0 : o0 + PIECE_O, :])
+                rows = raw[:].rearrange(
+                    "p o (q h w i j) -> p (o q) h w i j", q=PACK, h=SIDE, w=SIDE, i=KSIDE, j=KSIDE
+                )
+                r0 = piece * PIECE_O * PACK
+                for h, w in places:
+                    i0, i1 = valid_taps(h)
+                    j0, j1 = valid_taps(w)
+                    src = rows[:, :, h, w, i0:i1, j0:j1].rearrange("p r i j -> p i r j")
+                    dst = grouped[(h, w)][:, :, :, r0 : r0 + PIECE_O * PACK].rearrange("p i j r -> p i r j")
+                    if w % 2 == 0:
+                        nc.scalar.copy(out=dst, in_=src)
+                    else:
+                        nc.vector.tensor_copy(out=dst, in_=src)
+
+            half = slice((sub % 2) * SUB_O, (sub % 2 + 1) * SUB_O)
+            for h, w in places:
+                i0, i1 = valid_taps(h)
+                j0, j1 = valid_taps(w)
+                for i in range(i1 - i0):
+                    for j in range(j1 - j0):
+                        nc.vector.quantize_mx(
+                            out=w_codes[(h, w)][:, i, j, half].bitcast(FP8X4),
+                            scales=w_scales[(h, w)][:, i, j, half],
+                            in_=grouped[(h, w)][:, i, j, :],
+                        )
+            if sub % 2 == 0:
+                continue
+
+            o_first = (sub // 2) * WINDOW_O
+            result = work.tile([P, WINDOW_O, PLACES], F32, bufs=1)
+            for h in range(SIDE):
+                i0, i1 = valid_taps(h)
+                acc = psum.tile([P, SIDE, WINDOW_O], F32)
+                for w in range(SIDE):
+                    j0, j1 = valid_taps(w)
+                    taps = [(i, j) for i in range(i0, i1) for j in range(j0, j1)]
+                    for i, j in taps:
+                        x_place = (h + i - PAD) * SIDE + (w + j - PAD)
+                        nc.tensor.matmul_mx(
+                            out=acc[:, w, :],
+                            lhsT=x_codes[:, x_place, :].bitcast(FP8X4),
+                            lhsT_scale=x_scales[:, x_place, :],
+                            rhs=w_codes[(h, w)][:, i - i0, j - j0, :].bitcast(FP8X4),
+                            rhs_scale=w_scales[(h, w)][:, i - i0, j - j0, :],
+                            start=((i, j) == taps[0]),
+                            stop=((i, j) == taps[-1]),
+                        )
+                row = slice(h * SIDE, (h + 1) * SIDE)
+                biased = work.tile([P, WINDOW_O, SIDE], F32)
+                nc.vector.tensor_tensor(
+                    out=biased[:],
+                    in0=acc[:].rearrange("p w o -> p o w"),
+                    in1=bias_all[:, o_first : o_first + WINDOW_O, row],
+                    op=ALU.add,
+                )
+                nc.vector.scalar_tensor_tensor(
+                    out=result[:, :, row],
+                    in0=biased[:],
+                    scalar=NEG_SLOPE,
+                    in1=biased[:],
+                    op0=ALU.mult,
+                    op1=ALU.max,
+                )
+            for d in range(2):
+                o_part = slice(d * SUB_O, (d + 1) * SUB_O)
+                nc.sync.dma_start(
+                    out=out_rows[:, o_first + d * SUB_O : o_first + (d + 1) * SUB_O, :],
+                    in_=result[d * BATCH : (d + 1) * BATCH, o_part, :],
+                )

@@ -20,6 +20,7 @@ KSIDE = 3
 PAD = 1
 COLS = PLACES * KSIDE * KSIDE
 NEG_SLOPE = 0.1
+BANK = 512
 
 PIECE_O = 16
 SUB_O = 64
@@ -61,11 +62,21 @@ def tile_locallyconnected2d_kernel(tc, x, weight, bias, out):
                 in_=x_grouped[:, some, :, :, :].rearrange("p s d n q -> p (s d n q)"),
             )
 
+        bias_row = keep.tile([P, C_OUT * PLACES], BF16)
+        nc.gpsimd.memset(bias_row[:], 0.0)
+        nc.sync.dma_start(out=bias_row[0:1, :], in_=bias.rearrange("u o a b -> u (o a b)"))
+        ones = keep.tile([P, P], BF16)
+        nc.vector.memset(ones[:], 1.0)
         bias_all = keep.tile([P, C_OUT, PLACES], BF16)
-        nc.sync.dma_start(
-            out=bias_all[:].rearrange("p o s -> p (o s)"),
-            in_=bias.rearrange("u o a b -> (u o a b)").partition_broadcast(P),
-        )
+        bias_flat = bias_all[:].rearrange("p o s -> p (o s)")
+        for g in range(C_OUT * PLACES // BANK):
+            cols = slice(g * BANK, (g + 1) * BANK)
+            spread = psum.tile([P, BANK], F32, tag="acc")
+            nc.tensor.matmul(out=spread[:], lhsT=ones[:], rhs=bias_row[:, cols], start=True, stop=True)
+            if g % 2 == 0:
+                nc.scalar.copy(out=bias_flat[:, cols], in_=spread[:])
+            else:
+                nc.vector.tensor_copy(out=bias_flat[:, cols], in_=spread[:])
 
         grouped = {}
         w_codes = {}
@@ -123,7 +134,7 @@ def tile_locallyconnected2d_kernel(tc, x, weight, bias, out):
             result = work.tile([P, WINDOW_O, PLACES], F32, bufs=1)
             for h in range(SIDE):
                 i0, i1 = valid_taps(h)
-                acc = psum.tile([P, SIDE, WINDOW_O], F32)
+                acc = psum.tile([P, SIDE, WINDOW_O], F32, tag="acc")
                 for w in range(SIDE):
                     j0, j1 = valid_taps(w)
                     taps = [(i, j) for i in range(i0, i1) for j in range(j0, j1)]

@@ -7,6 +7,7 @@ BF16 = mybir.dt.bfloat16
 F32 = mybir.dt.float32
 U32 = mybir.dt.uint32
 U8 = mybir.dt.uint8
+I32 = mybir.dt.int32
 ALU = mybir.AluOpType
 
 P = 128
@@ -24,7 +25,6 @@ BANK = 512
 
 PIECE_O = 16
 SUB_O = 64
-WINDOW_O = 128
 PIECES = SUB_O // PIECE_O
 SUBS = C_OUT // SUB_O
 SUB_ROWS = SUB_O * PACK
@@ -37,14 +37,36 @@ def valid_taps(place):
     return max(0, PAD - place), min(KSIDE, SIDE + PAD - place)
 
 
+N_GROUPS = 10
+GROUP_BLOCKS = 12
+BLOCKS = N_GROUPS * GROUP_BLOCKS
+
+
+def block_of(w, j):
+    pair = w // 2
+    return 6 * pair + 2 * (w + j - PAD - pair) + w % 2
+
+
+def filled_runs(empty_blocks):
+    filled = [b for b in range(BLOCKS) if b % GROUP_BLOCKS not in empty_blocks]
+    starts = [b for b in filled if b - 1 not in filled]
+    return [(first, min(e for e in range(first + 1, BLOCKS + 1) if e not in filled)) for first in starts]
+
+
+VECTOR_PLACES = ((1, 1), (1, 2), (2, 1), (2, 2), (0, 1))
+
+
 def tile_locallyconnected2d_kernel(tc, x, weight, bias, out):
     nc = tc.nc
     places = [(h, w) for h in range(SIDE) for w in range(SIDE)]
+    GROUPS = [(h, i) for h in range(SIDE) for i in range(*valid_taps(h))]
+    EMPTY_BLOCKS = (block_of(0, KSIDE), block_of(SIDE - 1, -1))
+    FILLED_RUNS = filled_runs(EMPTY_BLOCKS)
     with ExitStack() as ctx:
-        stage = ctx.enter_context(tc.tile_pool(name="stage", bufs=4))
+        stage = ctx.enter_context(tc.tile_pool(name="stage", bufs=5))
         keep = ctx.enter_context(tc.tile_pool(name="keep", bufs=1))
         work = ctx.enter_context(tc.tile_pool(name="work", bufs=2))
-        psum = ctx.enter_context(tc.psum_pool(name="psum", bufs=4))
+        psum = ctx.enter_context(tc.psum_pool(name="psum", bufs=8))
 
         x_raw = stage.tile([P, BATCH, PACK * PLACES], BF16, tag="stage", align_bytes=64)
         nc.sync.dma_start(out=x_raw[:], in_=x.rearrange("n (p q) a b -> p n (q a b)", q=PACK))
@@ -78,21 +100,15 @@ def tile_locallyconnected2d_kernel(tc, x, weight, bias, out):
             else:
                 nc.vector.tensor_copy(out=bias_flat[:, cols], in_=spread[:])
 
-        grouped = {}
-        w_codes = {}
-        w_scales = {}
-        for h, w in places:
-            i0, i1 = valid_taps(h)
-            j0, j1 = valid_taps(w)
-            grouped[(h, w)] = keep.tile(
-                [P, i1 - i0, j1 - j0, SUB_ROWS], BF16, name="grouped_%d%d" % (h, w), align_bytes=64
-            )
-            w_codes[(h, w)] = keep.tile(
-                [P, i1 - i0, j1 - j0, WINDOW_O], U32, name="w_codes_%d%d" % (h, w), align_bytes=64
-            )
-            w_scales[(h, w)] = keep.tile(
-                [P, i1 - i0, j1 - j0, WINDOW_O], U8, name="w_scales_%d%d" % (h, w), align_bytes=64
-            )
+        grouped = keep.tile([P, BLOCKS, SUB_ROWS], BF16, align_bytes=64)
+        w_codes = keep.tile([P, BLOCKS, SUB_O], U32, align_bytes=64)
+        w_scales = keep.tile([P, BLOCKS, SUB_O], U8, align_bytes=64)
+        grouped_by_group = grouped[:].rearrange("p (g b) r -> p g b r", b=GROUP_BLOCKS)
+        codes_words = w_codes[:].bitcast(I32).rearrange("p (g b) o -> p g b o", b=GROUP_BLOCKS)
+        scale_words = w_scales[:].bitcast(I32).rearrange("p (g b) o -> p g b o", b=GROUP_BLOCKS)
+        for b in EMPTY_BLOCKS:
+            nc.vector.memset(codes_words[:, :, b, :], 0)
+            nc.vector.memset(scale_words[:, :, b, :], 0)
 
         w_rows = weight.rearrange("u o (p q) h w t -> p (u o) (q h w t)", q=PACK)
         out_rows = out.rearrange("n o a b -> n o (a b)")
@@ -109,65 +125,68 @@ def tile_locallyconnected2d_kernel(tc, x, weight, bias, out):
                 for h, w in places:
                     i0, i1 = valid_taps(h)
                     j0, j1 = valid_taps(w)
+                    g0 = GROUPS.index((h, i0))
+                    b0 = block_of(w, j0)
                     src = rows[:, :, h, w, i0:i1, j0:j1].rearrange("p r i j -> p i r j")
-                    dst = grouped[(h, w)][:, :, :, r0 : r0 + PIECE_O * PACK].rearrange("p i j r -> p i r j")
-                    if w % 2 == 0:
-                        nc.scalar.copy(out=dst, in_=src)
-                    else:
+                    dst = grouped_by_group[
+                        :, g0 : g0 + i1 - i0, b0 : b0 + 2 * (j1 - j0) - 1 : 2, r0 : r0 + PIECE_O * PACK
+                    ].rearrange("p i j r -> p i r j")
+                    if (h, w) in VECTOR_PLACES:
                         nc.vector.tensor_copy(out=dst, in_=src)
+                    else:
+                        nc.scalar.copy(out=dst, in_=src)
 
-            half = slice((sub % 2) * SUB_O, (sub % 2 + 1) * SUB_O)
-            for h, w in places:
-                i0, i1 = valid_taps(h)
-                j0, j1 = valid_taps(w)
-                for i in range(i1 - i0):
-                    for j in range(j1 - j0):
-                        nc.vector.quantize_mx(
-                            out=w_codes[(h, w)][:, i, j, half].bitcast(FP8X4),
-                            scales=w_scales[(h, w)][:, i, j, half],
-                            in_=grouped[(h, w)][:, i, j, :],
-                        )
-            if sub % 2 == 0:
-                continue
+            for first, last in FILLED_RUNS:
+                nc.vector.quantize_mx(
+                    out=w_codes[:, first:last, :].rearrange("p b o -> p (b o)").bitcast(FP8X4),
+                    scales=w_scales[:, first:last, :].rearrange("p b o -> p (b o)"),
+                    in_=grouped[:, first:last, :].rearrange("p b r -> p (b r)"),
+                )
 
-            o_first = (sub // 2) * WINDOW_O
-            result = work.tile([P, WINDOW_O, PLACES], F32, bufs=1)
-            for h in range(SIDE):
-                i0, i1 = valid_taps(h)
-                acc = psum.tile([P, SIDE, WINDOW_O], F32, tag="acc")
-                for w in range(SIDE):
-                    j0, j1 = valid_taps(w)
-                    taps = [(i, j) for i in range(i0, i1) for j in range(j0, j1)]
-                    for i, j in taps:
-                        x_place = (h + i - PAD) * SIDE + (w + j - PAD)
-                        nc.tensor.matmul_mx(
-                            out=acc[:, w, :],
-                            lhsT=x_codes[:, x_place, :].bitcast(FP8X4),
-                            lhsT_scale=x_scales[:, x_place, :],
-                            rhs=w_codes[(h, w)][:, i - i0, j - j0, :].bitcast(FP8X4),
-                            rhs_scale=w_scales[(h, w)][:, i - i0, j - j0, :],
-                            start=((i, j) == taps[0]),
-                            stop=((i, j) == taps[-1]),
-                        )
-                row = slice(h * SIDE, (h + 1) * SIDE)
-                biased = work.tile([P, WINDOW_O, SIDE], F32)
+            o_first = sub * SUB_O
+            banks = []
+            for top in range(0, SIDE, 2):
+                acc = psum.tile([P, 2 * SIDE, SUB_O], F32, tag="acc")
+                banks.append(acc)
+                for h in (top, top + 1):
+                    i0, i1 = valid_taps(h)
+                    for pair in range(SIDE // 2):
+                        first_place = (h - top) * SIDE + 2 * pair
+                        passes = [(i, step) for i in range(i0, i1) for step in range(KSIDE)]
+                        for i, step in passes:
+                            x_place = (h + i - PAD) * SIDE + pair + step
+                            b = GROUPS.index((h, i)) * GROUP_BLOCKS + 6 * pair + 2 * step
+                            nc.tensor.matmul_mx(
+                                out=acc[:, first_place : first_place + 2, :].rearrange("p k o -> p (k o)"),
+                                lhsT=x_codes[:, x_place, :].bitcast(FP8X4),
+                                lhsT_scale=x_scales[:, x_place, :],
+                                rhs=w_codes[:, b : b + 2, :].rearrange("p b o -> p (b o)").bitcast(FP8X4),
+                                rhs_scale=w_scales[:, b : b + 2, :].rearrange("p b o -> p (b o)"),
+                                start=((i, step) == passes[0]),
+                                stop=((i, step) == passes[-1]),
+                            )
+
+            result = work.tile([P, SUB_O, PLACES], F32)
+            for k, acc in enumerate(banks):
+                some = slice(k * 2 * SIDE, (k + 1) * 2 * SIDE)
+                biased = work.tile([P, SUB_O, 2 * SIDE], F32)
                 nc.vector.tensor_tensor(
                     out=biased[:],
-                    in0=acc[:].rearrange("p w o -> p o w"),
-                    in1=bias_all[:, o_first : o_first + WINDOW_O, row],
+                    in0=acc[:].rearrange("p k o -> p o k"),
+                    in1=bias_all[:, o_first : o_first + SUB_O, some],
                     op=ALU.add,
                 )
                 nc.vector.scalar_tensor_tensor(
-                    out=result[:, :, row],
+                    out=result[:, :, some],
                     in0=biased[:],
                     scalar=NEG_SLOPE,
                     in1=biased[:],
                     op0=ALU.mult,
                     op1=ALU.max,
                 )
+            half_o = SUB_O // 2
             for d in range(2):
-                o_part = slice(d * SUB_O, (d + 1) * SUB_O)
                 nc.sync.dma_start(
-                    out=out_rows[:, o_first + d * SUB_O : o_first + (d + 1) * SUB_O, :],
-                    in_=result[d * BATCH : (d + 1) * BATCH, o_part, :],
+                    out=out_rows[:, o_first + d * half_o : o_first + (d + 1) * half_o, :],
+                    in_=result[d * BATCH : (d + 1) * BATCH, d * half_o : (d + 1) * half_o, :],
                 )

@@ -24,9 +24,10 @@ NEG_SLOPE = 0.1
 BANK = 512
 
 PIECE_O = 16
-SUB_O = 64
-PIECES = SUB_O // PIECE_O
+SUB_O = 32
 SUBS = C_OUT // SUB_O
+LOADS = (PIECE_O, PIECE_O)
+LAST_LOADS = (PIECE_O, PIECE_O // 2, PIECE_O // 2)
 SUB_ROWS = SUB_O * PACK
 
 VALID_TAPS = 100
@@ -40,17 +41,13 @@ def valid_taps(place):
 N_GROUPS = 10
 GROUP_BLOCKS = 12
 BLOCKS = N_GROUPS * GROUP_BLOCKS
+PASS_BLOCKS = 4
+QUANTISE_BLOCKS = (32, 32, 32, 16, 8)
 
 
 def block_of(w, j):
     pair = w // 2
     return 6 * pair + 2 * (w + j - PAD - pair) + w % 2
-
-
-def filled_runs(empty_blocks):
-    filled = [b for b in range(BLOCKS) if b % GROUP_BLOCKS not in empty_blocks]
-    starts = [b for b in filled if b - 1 not in filled]
-    return [(first, min(e for e in range(first + 1, BLOCKS + 1) if e not in filled)) for first in starts]
 
 
 VECTOR_PLACES = ((1, 1), (1, 2), (2, 1), (2, 2), (0, 1))
@@ -61,12 +58,12 @@ def tile_locallyconnected2d_kernel(tc, x, weight, bias, out):
     places = [(h, w) for h in range(SIDE) for w in range(SIDE)]
     GROUPS = [(h, i) for h in range(SIDE) for i in range(*valid_taps(h))]
     EMPTY_BLOCKS = (block_of(0, KSIDE), block_of(SIDE - 1, -1))
-    FILLED_RUNS = filled_runs(EMPTY_BLOCKS)
     with ExitStack() as ctx:
-        stage = ctx.enter_context(tc.tile_pool(name="stage", bufs=5))
+        stage = ctx.enter_context(tc.tile_pool(name="stage", bufs=6))
         keep = ctx.enter_context(tc.tile_pool(name="keep", bufs=1))
         work = ctx.enter_context(tc.tile_pool(name="work", bufs=2))
         psum = ctx.enter_context(tc.psum_pool(name="psum", bufs=8))
+        ctx.enter_context(tc.manual_schedule(engines={mybir.EngineType.SP}))
 
         x_raw = stage.tile([P, BATCH, PACK * PLACES], BF16, tag="stage", align_bytes=64)
         nc.sync.dma_start(out=x_raw[:], in_=x.rearrange("n (p q) a b -> p n (q a b)", q=PACK))
@@ -100,80 +97,91 @@ def tile_locallyconnected2d_kernel(tc, x, weight, bias, out):
             else:
                 nc.vector.tensor_copy(out=bias_flat[:, cols], in_=spread[:])
 
-        grouped = keep.tile([P, BLOCKS, SUB_ROWS], BF16, align_bytes=64)
-        w_codes = keep.tile([P, BLOCKS, SUB_O], U32, align_bytes=64)
-        w_scales = keep.tile([P, BLOCKS, SUB_O], U8, align_bytes=64)
-        grouped_by_group = grouped[:].rearrange("p (g b) r -> p g b r", b=GROUP_BLOCKS)
-        codes_words = w_codes[:].bitcast(I32).rearrange("p (g b) o -> p g b o", b=GROUP_BLOCKS)
-        scale_words = w_scales[:].bitcast(I32).rearrange("p (g b) o -> p g b o", b=GROUP_BLOCKS)
-        for b in EMPTY_BLOCKS:
-            nc.vector.memset(codes_words[:, :, b, :], 0)
-            nc.vector.memset(scale_words[:, :, b, :], 0)
+        grouped = [
+            keep.tile([P, BLOCKS, SUB_ROWS], BF16, name="grouped_%d" % k, align_bytes=64) for k in range(2)
+        ]
+        for k in range(2):
+            for b in EMPTY_BLOCKS:
+                nc.vector.memset(
+                    grouped[k][:].rearrange("p (g b) r -> p g b r", b=GROUP_BLOCKS)[:, :, b, :].bitcast(I32), 0
+                )
+        spare = PASS_BLOCKS - 2
+        w_codes = keep.tile([P, BLOCKS + spare, SUB_O], U32, align_bytes=64)
+        w_scales = keep.tile([P, BLOCKS + spare, SUB_O], U8, align_bytes=64)
+        nc.vector.memset(w_codes[:, BLOCKS:, :].rearrange("p b o -> p (b o)").bitcast(I32), 0)
+        nc.vector.memset(w_scales[:, BLOCKS:, :].rearrange("p b o -> p (b o)").bitcast(I32), 0)
 
         w_rows = weight.rearrange("u o (p q) h w t -> p (u o) (q h w t)", q=PACK)
         out_rows = out.rearrange("n o a b -> n o (a b)")
 
+        results = []
         for sub in range(SUBS):
-            for piece in range(PIECES):
-                o0 = sub * SUB_O + piece * PIECE_O
-                raw = stage.tile([P, PIECE_O, PACK * COLS], BF16, tag="stage", align_bytes=64)
-                nc.sync.dma_start(out=raw[:], in_=w_rows[:, o0 : o0 + PIECE_O, :])
+            o_first = sub * SUB_O
+            blocks = grouped[sub % 2]
+            by_group = blocks[:].rearrange("p (g b) r -> p g b r", b=GROUP_BLOCKS)
+            o0 = o_first
+            for piece_o in LAST_LOADS if sub == SUBS - 1 else LOADS:
+                raw = stage.tile([P, piece_o, PACK * COLS], BF16, tag="stage", align_bytes=64)
+                nc.sync.dma_start(out=raw[:], in_=w_rows[:, o0 : o0 + piece_o, :])
                 rows = raw[:].rearrange(
                     "p o (q h w i j) -> p (o q) h w i j", q=PACK, h=SIDE, w=SIDE, i=KSIDE, j=KSIDE
                 )
-                r0 = piece * PIECE_O * PACK
+                r0 = (o0 - o_first) * PACK
                 for h, w in places:
                     i0, i1 = valid_taps(h)
                     j0, j1 = valid_taps(w)
                     g0 = GROUPS.index((h, i0))
                     b0 = block_of(w, j0)
                     src = rows[:, :, h, w, i0:i1, j0:j1].rearrange("p r i j -> p i r j")
-                    dst = grouped_by_group[
-                        :, g0 : g0 + i1 - i0, b0 : b0 + 2 * (j1 - j0) - 1 : 2, r0 : r0 + PIECE_O * PACK
+                    dst = by_group[
+                        :, g0 : g0 + i1 - i0, b0 : b0 + 2 * (j1 - j0) - 1 : 2, r0 : r0 + piece_o * PACK
                     ].rearrange("p i j r -> p i r j")
                     if (h, w) in VECTOR_PLACES:
                         nc.vector.tensor_copy(out=dst, in_=src)
                     else:
                         nc.scalar.copy(out=dst, in_=src)
+                o0 += piece_o
 
-            for first, last in FILLED_RUNS:
+            first = 0
+            for n_blocks in QUANTISE_BLOCKS:
+                some = slice(first, first + n_blocks)
                 nc.vector.quantize_mx(
-                    out=w_codes[:, first:last, :].rearrange("p b o -> p (b o)").bitcast(FP8X4),
-                    scales=w_scales[:, first:last, :].rearrange("p b o -> p (b o)"),
-                    in_=grouped[:, first:last, :].rearrange("p b r -> p (b r)"),
+                    out=w_codes[:, some, :].rearrange("p b o -> p (b o)").bitcast(FP8X4),
+                    scales=w_scales[:, some, :].rearrange("p b o -> p (b o)"),
+                    in_=blocks[:, some, :].rearrange("p b r -> p (b r)"),
                 )
+                first += n_blocks
 
-            o_first = sub * SUB_O
             banks = []
             for top in range(0, SIDE, 2):
-                acc = psum.tile([P, 2 * SIDE, SUB_O], F32, tag="acc")
+                acc = psum.tile([P, SIDE, PASS_BLOCKS * SUB_O], F32, tag="acc")
                 banks.append(acc)
                 for h in (top, top + 1):
                     i0, i1 = valid_taps(h)
                     for pair in range(SIDE // 2):
-                        first_place = (h - top) * SIDE + 2 * pair
                         passes = [(i, step) for i in range(i0, i1) for step in range(KSIDE)]
                         for i, step in passes:
                             x_place = (h + i - PAD) * SIDE + pair + step
                             b = GROUPS.index((h, i)) * GROUP_BLOCKS + 6 * pair + 2 * step
                             nc.tensor.matmul_mx(
-                                out=acc[:, first_place : first_place + 2, :].rearrange("p k o -> p (k o)"),
+                                out=acc[:, (h - top) * 2 + pair, :],
                                 lhsT=x_codes[:, x_place, :].bitcast(FP8X4),
                                 lhsT_scale=x_scales[:, x_place, :],
-                                rhs=w_codes[:, b : b + 2, :].rearrange("p b o -> p (b o)").bitcast(FP8X4),
-                                rhs_scale=w_scales[:, b : b + 2, :].rearrange("p b o -> p (b o)"),
+                                rhs=w_codes[:, b : b + PASS_BLOCKS, :].rearrange("p b o -> p (b o)").bitcast(FP8X4),
+                                rhs_scale=w_scales[:, b : b + PASS_BLOCKS, :].rearrange("p b o -> p (b o)"),
                                 start=((i, step) == passes[0]),
                                 stop=((i, step) == passes[-1]),
                             )
 
-            result = work.tile([P, SUB_O, PLACES], F32)
+            result = keep.tile([P, SUB_O, PLACES], F32, name="result_%d" % sub)
+            results.append(result)
             for k, acc in enumerate(banks):
                 some = slice(k * 2 * SIDE, (k + 1) * 2 * SIDE)
                 biased = work.tile([P, SUB_O, 2 * SIDE], F32)
                 nc.vector.tensor_tensor(
-                    out=biased[:],
-                    in0=acc[:].rearrange("p k o -> p o k"),
-                    in1=bias_all[:, o_first : o_first + SUB_O, some],
+                    out=biased[:].rearrange("p o (r e) -> p o r e", e=2),
+                    in0=acc[:, :, 0 : 2 * SUB_O].rearrange("p r (e o) -> p o r e", e=2),
+                    in1=bias_all[:, o_first : o_first + SUB_O, some].rearrange("p o (r e) -> p o r e", e=2),
                     op=ALU.add,
                 )
                 nc.vector.scalar_tensor_tensor(
@@ -184,9 +192,12 @@ def tile_locallyconnected2d_kernel(tc, x, weight, bias, out):
                     op0=ALU.mult,
                     op1=ALU.max,
                 )
-            half_o = SUB_O // 2
+
+        half_o = SUB_O // 2
+        for sub, result in enumerate(results):
             for d in range(2):
+                o0 = sub * SUB_O + d * half_o
                 nc.sync.dma_start(
-                    out=out_rows[:, o_first + d * half_o : o_first + (d + 1) * half_o, :],
+                    out=out_rows[:, o0 : o0 + half_o, :],
                     in_=result[d * BATCH : (d + 1) * BATCH, d * half_o : (d + 1) * half_o, :],
                 )

@@ -42,7 +42,7 @@ N_GROUPS = 10
 GROUP_BLOCKS = 12
 BLOCKS = N_GROUPS * GROUP_BLOCKS
 PASS_BLOCKS = 4
-QUANTISE_BLOCKS = (32, 32, 32, 16, 8)
+QUANTISE_BLOCKS = (8, 16, 32, 32, 16, 8, 8)
 
 
 def block_of(w, j):

@@ -51,6 +51,8 @@ def block_of(w, j):
 
 
 VECTOR_PLACES = ((1, 1), (1, 2), (2, 1), (2, 2), (0, 1))
+LAST_VECTOR_PLACES = VECTOR_PLACES + ((0, 2), (1, 0), (2, 0), (1, 3))
+X_VECTOR = 10
 
 
 def tile_locallyconnected2d_kernel(tc, x, weight, bias, out):
@@ -65,20 +67,23 @@ def tile_locallyconnected2d_kernel(tc, x, weight, bias, out):
         psum = ctx.enter_context(tc.psum_pool(name="psum", bufs=8))
         ctx.enter_context(tc.manual_schedule(engines={mybir.EngineType.SP}))
 
-        x_raw = stage.tile([P, BATCH, PACK * PLACES], BF16, tag="stage", align_bytes=64)
+        x_raw = stage.tile([P, BATCH, PACK * PLACES], BF16, tag="stage", align_bytes=256)
         nc.sync.dma_start(out=x_raw[:], in_=x.rearrange("n (p q) a b -> p n (q a b)", q=PACK))
-        x_grouped = stage.tile([P, PLACES, 2, BATCH, PACK], BF16, tag="stage", align_bytes=64)
+        x_grouped = stage.tile([P, PLACES, BATCH, PACK], BF16, tag="stage", align_bytes=256)
         x_by_place = x_raw[:].rearrange("p n (q s) -> p s n q", q=PACK)
-        nc.vector.tensor_copy(out=x_grouped[:, :, 0, :, :], in_=x_by_place)
-        nc.scalar.copy(out=x_grouped[:, :, 1, :, :], in_=x_by_place)
-        x_codes = keep.tile([P, PLACES, 2 * BATCH], U32, align_bytes=64)
-        x_scales = keep.tile([P, PLACES, 2 * BATCH], U8, align_bytes=64)
+        for some in (slice(0, X_VECTOR // 2), slice(X_VECTOR // 2, X_VECTOR)):
+            nc.vector.tensor_copy(out=x_grouped[:, some, :, :], in_=x_by_place[:, some, :, :])
+        nc.scalar.copy(out=x_grouped[:, X_VECTOR:, :, :], in_=x_by_place[:, X_VECTOR:, :, :])
+        x_codes = keep.tile([P, PLACES + 1, BATCH], U32, align_bytes=64)
+        x_scales = keep.tile([P, PLACES + 1, BATCH], U8, align_bytes=64)
+        nc.gpsimd.memset(x_codes[:, PLACES, :].bitcast(I32), 0)
+        nc.gpsimd.memset(x_scales[:, PLACES, :].bitcast(I32), 0)
         for lo in range(0, PLACES, PLACES // 2):
             some = slice(lo, lo + PLACES // 2)
             nc.vector.quantize_mx(
                 out=x_codes[:, some, :].rearrange("p s m -> p (s m)").bitcast(FP8X4),
                 scales=x_scales[:, some, :].rearrange("p s m -> p (s m)"),
-                in_=x_grouped[:, some, :, :, :].rearrange("p s d n q -> p (s d n q)"),
+                in_=x_grouped[:, some, :, :].rearrange("p s n q -> p (s n q)"),
             )
 
         bias_row = keep.tile([P, C_OUT * PLACES], BF16)
@@ -121,7 +126,7 @@ def tile_locallyconnected2d_kernel(tc, x, weight, bias, out):
             by_group = blocks[:].rearrange("p (g b) r -> p g b r", b=GROUP_BLOCKS)
             o0 = o_first
             for piece_o in LAST_LOADS if sub == SUBS - 1 else LOADS:
-                raw = stage.tile([P, piece_o, PACK * COLS], BF16, tag="stage", align_bytes=64)
+                raw = stage.tile([P, piece_o, PACK * COLS], BF16, tag="stage", align_bytes=256)
                 nc.sync.dma_start(out=raw[:], in_=w_rows[:, o0 : o0 + piece_o, :])
                 rows = raw[:].rearrange(
                     "p o (q h w i j) -> p (o q) h w i j", q=PACK, h=SIDE, w=SIDE, i=KSIDE, j=KSIDE
@@ -136,7 +141,8 @@ def tile_locallyconnected2d_kernel(tc, x, weight, bias, out):
                     dst = by_group[
                         :, g0 : g0 + i1 - i0, b0 : b0 + 2 * (j1 - j0) - 1 : 2, r0 : r0 + piece_o * PACK
                     ].rearrange("p i j r -> p i r j")
-                    if (h, w) in VECTOR_PLACES:
+                    last = o0 + piece_o == C_OUT
+                    if (h, w) in (LAST_VECTOR_PLACES if last else VECTOR_PLACES):
                         nc.vector.tensor_copy(out=dst, in_=src)
                     else:
                         nc.scalar.copy(out=dst, in_=src)
@@ -165,8 +171,8 @@ def tile_locallyconnected2d_kernel(tc, x, weight, bias, out):
                             b = GROUPS.index((h, i)) * GROUP_BLOCKS + 6 * pair + 2 * step
                             nc.tensor.matmul_mx(
                                 out=acc[:, (h - top) * 2 + pair, :],
-                                lhsT=x_codes[:, x_place, :].bitcast(FP8X4),
-                                lhsT_scale=x_scales[:, x_place, :],
+                                lhsT=x_codes[:, x_place : x_place + 2, :].rearrange("p s m -> p (s m)").bitcast(FP8X4),
+                                lhsT_scale=x_scales[:, x_place : x_place + 2, :].rearrange("p s m -> p (s m)"),
                                 rhs=w_codes[:, b : b + PASS_BLOCKS, :].rearrange("p b o -> p (b o)").bitcast(FP8X4),
                                 rhs_scale=w_scales[:, b : b + PASS_BLOCKS, :].rearrange("p b o -> p (b o)"),
                                 start=((i, step) == passes[0]),
@@ -193,11 +199,5 @@ def tile_locallyconnected2d_kernel(tc, x, weight, bias, out):
                     op1=ALU.max,
                 )
 
-        half_o = SUB_O // 2
         for sub, result in enumerate(results):
-            for d in range(2):
-                o0 = sub * SUB_O + d * half_o
-                nc.sync.dma_start(
-                    out=out_rows[:, o0 : o0 + half_o, :],
-                    in_=result[d * BATCH : (d + 1) * BATCH, d * half_o : (d + 1) * half_o, :],
-                )
+            nc.sync.dma_start(out=out_rows[:, sub * SUB_O : (sub + 1) * SUB_O, :], in_=result[0:BATCH, :, :])

@@ -27,7 +27,7 @@ PIECE_O = 16
 SUB_O = 32
 SUBS = C_OUT // SUB_O
 LOADS = (PIECE_O, PIECE_O)
-LAST_LOADS = (PIECE_O, PIECE_O // 2, PIECE_O // 2)
+LAST_LOADS = (PIECE_O, PIECE_O // 2, PIECE_O // 4, PIECE_O // 4)
 SUB_ROWS = SUB_O * PACK
 
 VALID_TAPS = 100
@@ -45,27 +45,81 @@ PASS_BLOCKS = 4
 QUANTISE_BLOCKS = (8, 16, 32, 32, 16, 8, 8)
 
 
+EMPTY_BLOCKS = (2, 9)
+BLOCK_STEP = SIDE
+
+
 def block_of(w, j):
-    pair = w // 2
-    return 6 * pair + 2 * (w + j - PAD - pair) + w % 2
+    x_col = w + j - PAD
+    return BLOCK_STEP * x_col + 1 - w
 
 
-VECTOR_PLACES = ((1, 1), (1, 2), (2, 1), (2, 2), (0, 1))
-LAST_VECTOR_PLACES = VECTOR_PLACES + ((0, 2), (1, 0), (2, 0), (1, 3))
+LEFT = 2
+ROW_BLOCKS = SIDE + 4
+WINDOWS = ((0, 0, LEFT + 2), (3, 8, 0), (1, 2, LEFT), (2, 6, LEFT))
+
+ROWS = ((0,), (1, 2), (3,))
+VECTOR_PLACES = (((1, 2), 1), ((1, 2), 2), ((0,), 1))
+LAST_VECTOR_PLACES = VECTOR_PLACES + (((0,), 2), ((1, 2), 0))
 X_VECTOR = 10
 
 
 def tile_locallyconnected2d_kernel(tc, x, weight, bias, out):
     nc = tc.nc
-    places = [(h, w) for h in range(SIDE) for w in range(SIDE)]
+    places = [(rows, w) for rows in ROWS for w in range(SIDE)]
     GROUPS = [(h, i) for h in range(SIDE) for i in range(*valid_taps(h))]
-    EMPTY_BLOCKS = (block_of(0, KSIDE), block_of(SIDE - 1, -1))
     with ExitStack() as ctx:
         stage = ctx.enter_context(tc.tile_pool(name="stage", bufs=6))
         keep = ctx.enter_context(tc.tile_pool(name="keep", bufs=1))
         work = ctx.enter_context(tc.tile_pool(name="work", bufs=2))
         psum = ctx.enter_context(tc.psum_pool(name="psum", bufs=8))
         ctx.enter_context(tc.manual_schedule(engines={mybir.EngineType.SP}))
+
+        grouped = [
+            keep.tile([P, BLOCKS, SUB_ROWS], BF16, name="grouped_%d" % k, align_bytes=64) for k in range(2)
+        ]
+        for k in range(2):
+            for b in EMPTY_BLOCKS:
+                nc.vector.memset(
+                    grouped[k][:].rearrange("p (g b) r -> p g b r", b=GROUP_BLOCKS)[:, :, b, :].bitcast(I32), 0
+                )
+        w_codes = keep.tile([P, BLOCKS, SUB_O], U32, align_bytes=64)
+        w_scales = keep.tile([P, BLOCKS, SUB_O], U8, align_bytes=64)
+
+        w_rows = weight.rearrange("u o (p q) h w t -> p (u o) (q h w t)", q=PACK)
+        out_rows = out.rearrange("n o a b -> n o (a b)")
+
+        def load(o0, piece_o):
+            raw = stage.tile([P, piece_o, PACK * COLS], BF16, tag="stage", align_bytes=256)
+            nc.sync.dma_start(out=raw[:], in_=w_rows[:, o0 : o0 + piece_o, :])
+            return raw
+
+        def lay_out(raw, o0, piece_o):
+            sub = o0 // SUB_O
+            by_group = grouped[sub % 2][:].rearrange("p (g b) r -> p g b r", b=GROUP_BLOCKS)
+            rows = raw[:].rearrange(
+                "p o (q h w i j) -> p (o q) h w i j", q=PACK, h=SIDE, w=SIDE, i=KSIDE, j=KSIDE
+            )
+            r0 = o0 % SUB_O * PACK
+            for tops, w in places:
+                i0, i1 = valid_taps(tops[0])
+                j0, j1 = valid_taps(w)
+                g0 = GROUPS.index((tops[0], i0))
+                b0 = block_of(w, j0)
+                src = rows[:, :, tops[0] : tops[-1] + 1, w, i0:i1, j0:j1].rearrange("p r h i j -> p h i r j")
+                dst = by_group[
+                    :,
+                    g0 : g0 + len(tops) * (i1 - i0),
+                    b0 : b0 + BLOCK_STEP * (j1 - j0 - 1) + 1 : BLOCK_STEP,
+                    r0 : r0 + piece_o * PACK,
+                ].rearrange("p (h i) j r -> p h i r j", h=len(tops))
+                if (tops, w) in (LAST_VECTOR_PLACES if sub == SUBS - 1 else VECTOR_PLACES):
+                    nc.vector.tensor_copy(out=dst, in_=src)
+                else:
+                    nc.scalar.copy(out=dst, in_=src)
+
+        first_raw = load(0, PIECE_O)
+        lay_out(first_raw, 0, PIECE_O)
 
         x_raw = stage.tile([P, BATCH, PACK * PLACES], BF16, tag="stage", align_bytes=256)
         nc.sync.dma_start(out=x_raw[:], in_=x.rearrange("n (p q) a b -> p n (q a b)", q=PACK))
@@ -93,59 +147,24 @@ def tile_locallyconnected2d_kernel(tc, x, weight, bias, out):
         nc.vector.memset(ones[:], 1.0)
         bias_all = keep.tile([P, C_OUT, PLACES], BF16)
         bias_flat = bias_all[:].rearrange("p o s -> p (o s)")
-        for g in range(C_OUT * PLACES // BANK):
-            cols = slice(g * BANK, (g + 1) * BANK)
-            spread = psum.tile([P, BANK], F32, tag="acc")
-            nc.tensor.matmul(out=spread[:], lhsT=ones[:], rhs=bias_row[:, cols], start=True, stop=True)
-            if g % 2 == 0:
-                nc.scalar.copy(out=bias_flat[:, cols], in_=spread[:])
-            else:
-                nc.vector.tensor_copy(out=bias_flat[:, cols], in_=spread[:])
-
-        grouped = [
-            keep.tile([P, BLOCKS, SUB_ROWS], BF16, name="grouped_%d" % k, align_bytes=64) for k in range(2)
-        ]
-        for k in range(2):
-            for b in EMPTY_BLOCKS:
-                nc.vector.memset(
-                    grouped[k][:].rearrange("p (g b) r -> p g b r", b=GROUP_BLOCKS)[:, :, b, :].bitcast(I32), 0
-                )
-        spare = PASS_BLOCKS - 2
-        w_codes = keep.tile([P, BLOCKS + spare, SUB_O], U32, align_bytes=64)
-        w_scales = keep.tile([P, BLOCKS + spare, SUB_O], U8, align_bytes=64)
-        nc.vector.memset(w_codes[:, BLOCKS:, :].rearrange("p b o -> p (b o)").bitcast(I32), 0)
-        nc.vector.memset(w_scales[:, BLOCKS:, :].rearrange("p b o -> p (b o)").bitcast(I32), 0)
-
-        w_rows = weight.rearrange("u o (p q) h w t -> p (u o) (q h w t)", q=PACK)
-        out_rows = out.rearrange("n o a b -> n o (a b)")
+        for g in range(C_OUT * PLACES // (2 * BANK)):
+            spread = psum.tile([P, 2, BANK], BF16, tag="acc")
+            first = g * 2 * BANK
+            for k in range(2):
+                cols = slice(first + k * BANK, first + (k + 1) * BANK)
+                nc.tensor.matmul(out=spread[:, k, :], lhsT=ones[:], rhs=bias_row[:, cols], start=True, stop=True)
+            nc.vector.tensor_copy(
+                out=bias_flat[:, first : first + 2 * BANK], in_=spread[:].rearrange("p k n -> p (k n)")
+            )
 
         results = []
         for sub in range(SUBS):
             o_first = sub * SUB_O
             blocks = grouped[sub % 2]
-            by_group = blocks[:].rearrange("p (g b) r -> p g b r", b=GROUP_BLOCKS)
             o0 = o_first
             for piece_o in LAST_LOADS if sub == SUBS - 1 else LOADS:
-                raw = stage.tile([P, piece_o, PACK * COLS], BF16, tag="stage", align_bytes=256)
-                nc.sync.dma_start(out=raw[:], in_=w_rows[:, o0 : o0 + piece_o, :])
-                rows = raw[:].rearrange(
-                    "p o (q h w i j) -> p (o q) h w i j", q=PACK, h=SIDE, w=SIDE, i=KSIDE, j=KSIDE
-                )
-                r0 = (o0 - o_first) * PACK
-                for h, w in places:
-                    i0, i1 = valid_taps(h)
-                    j0, j1 = valid_taps(w)
-                    g0 = GROUPS.index((h, i0))
-                    b0 = block_of(w, j0)
-                    src = rows[:, :, h, w, i0:i1, j0:j1].rearrange("p r i j -> p i r j")
-                    dst = by_group[
-                        :, g0 : g0 + i1 - i0, b0 : b0 + 2 * (j1 - j0) - 1 : 2, r0 : r0 + piece_o * PACK
-                    ].rearrange("p i j r -> p i r j")
-                    last = o0 + piece_o == C_OUT
-                    if (h, w) in (LAST_VECTOR_PLACES if last else VECTOR_PLACES):
-                        nc.vector.tensor_copy(out=dst, in_=src)
-                    else:
-                        nc.scalar.copy(out=dst, in_=src)
+                if o0 > 0:
+                    lay_out(load(o0, piece_o), o0, piece_o)
                 o0 += piece_o
 
             first = 0
@@ -160,44 +179,38 @@ def tile_locallyconnected2d_kernel(tc, x, weight, bias, out):
 
             banks = []
             for top in range(0, SIDE, 2):
-                acc = psum.tile([P, SIDE, PASS_BLOCKS * SUB_O], F32, tag="acc")
+                acc = psum.tile([P, 2, ROW_BLOCKS, SUB_O], F32, tag="acc")
                 banks.append(acc)
                 for h in (top, top + 1):
-                    i0, i1 = valid_taps(h)
-                    for pair in range(SIDE // 2):
-                        passes = [(i, step) for i in range(i0, i1) for step in range(KSIDE)]
-                        for i, step in passes:
-                            x_place = (h + i - PAD) * SIDE + pair + step
-                            b = GROUPS.index((h, i)) * GROUP_BLOCKS + 6 * pair + 2 * step
-                            nc.tensor.matmul_mx(
-                                out=acc[:, (h - top) * 2 + pair, :],
-                                lhsT=x_codes[:, x_place : x_place + 2, :].rearrange("p s m -> p (s m)").bitcast(FP8X4),
-                                lhsT_scale=x_scales[:, x_place : x_place + 2, :].rearrange("p s m -> p (s m)"),
-                                rhs=w_codes[:, b : b + PASS_BLOCKS, :].rearrange("p b o -> p (b o)").bitcast(FP8X4),
-                                rhs_scale=w_scales[:, b : b + PASS_BLOCKS, :].rearrange("p b o -> p (b o)"),
-                                start=((i, step) == passes[0]),
-                                stop=((i, step) == passes[-1]),
-                            )
+                    passes = [(i, window) for i in range(*valid_taps(h)) for window in WINDOWS]
+                    for i, window in passes:
+                        x_col, first_block, first_out = window
+                        x_place = (h + i - PAD) * SIDE + x_col
+                        b = GROUPS.index((h, i)) * GROUP_BLOCKS + first_block
+                        nc.tensor.matmul_mx(
+                            out=acc[:, h - top, first_out : first_out + PASS_BLOCKS, :].rearrange("p b o -> p (b o)"),
+                            lhsT=x_codes[:, x_place : x_place + 2, :].rearrange("p s m -> p (s m)").bitcast(FP8X4),
+                            lhsT_scale=x_scales[:, x_place : x_place + 2, :].rearrange("p s m -> p (s m)"),
+                            rhs=w_codes[:, b : b + PASS_BLOCKS, :].rearrange("p b o -> p (b o)").bitcast(FP8X4),
+                            rhs_scale=w_scales[:, b : b + PASS_BLOCKS, :].rearrange("p b o -> p (b o)"),
+                            start=((i, window) == passes[0]),
+                            stop=((i, window) == passes[-1]),
+                        )
 
             result = keep.tile([P, SUB_O, PLACES], F32, name="result_%d" % sub)
             results.append(result)
+            biased = work.tile([P, SUB_O, PLACES], F32)
             for k, acc in enumerate(banks):
                 some = slice(k * 2 * SIDE, (k + 1) * 2 * SIDE)
-                biased = work.tile([P, SUB_O, 2 * SIDE], F32)
                 nc.vector.tensor_tensor(
-                    out=biased[:].rearrange("p o (r e) -> p o r e", e=2),
-                    in0=acc[:, :, 0 : 2 * SUB_O].rearrange("p r (e o) -> p o r e", e=2),
-                    in1=bias_all[:, o_first : o_first + SUB_O, some].rearrange("p o (r e) -> p o r e", e=2),
+                    out=biased[:, :, some].rearrange("p o (r w) -> p o r w", w=SIDE),
+                    in0=acc[:, :, LEFT : LEFT + SIDE, :].rearrange("p r w o -> p o r w")[:, :, :, ::-1],
+                    in1=bias_all[:, o_first : o_first + SUB_O, some].rearrange("p o (r w) -> p o r w", w=SIDE),
                     op=ALU.add,
                 )
-                nc.vector.scalar_tensor_tensor(
-                    out=result[:, :, some],
-                    in0=biased[:],
-                    scalar=NEG_SLOPE,
-                    in1=biased[:],
-                    op0=ALU.mult,
-                    op1=ALU.max,
-                )
+            nc.vector.scalar_tensor_tensor(
+                out=result[:], in0=biased[:], scalar=NEG_SLOPE, in1=biased[:], op0=ALU.mult, op1=ALU.max
+            )
 
         for sub, result in enumerate(results):
             nc.sync.dma_start(out=out_rows[:, sub * SUB_O : (sub + 1) * SUB_O, :], in_=result[0:BATCH, :, :])

@@ -1,6 +1,7 @@
 from contextlib import ExitStack
 
 import concourse.mybir as mybir
+from concourse.masks import make_identity
 
 FP8X4 = mybir.dt.float8_e4m3fn_x4
 BF16 = mybir.dt.bfloat16
@@ -61,7 +62,7 @@ WINDOWS = ((0, 0, LEFT + 2), (3, 8, 0), (1, 2, LEFT), (2, 6, LEFT))
 ROWS = ((0,), (1, 2), (3,))
 VECTOR_PLACES = (((1, 2), 1), ((1, 2), 2), ((0,), 1))
 LAST_VECTOR_PLACES = VECTOR_PLACES + (((0,), 2), ((1, 2), 0))
-X_VECTOR = 10
+X_ROW = C_IN // 2 * PLACES
 
 
 def tile_locallyconnected2d_kernel(tc, x, weight, bias, out):
@@ -118,16 +119,33 @@ def tile_locallyconnected2d_kernel(tc, x, weight, bias, out):
                 else:
                     nc.scalar.copy(out=dst, in_=src)
 
+        half_p = P // 2
+        x_rows = stage.tile([P, 2, X_ROW], BF16, tag="stage", align_bytes=256)
+        nc.sync.dma_start(out=x_rows[:, 0, :], in_=x.rearrange("n (f c) a b -> (n f) (c a b)", f=2))
         first_raw = load(0, PIECE_O)
-        lay_out(first_raw, 0, PIECE_O)
-
-        x_raw = stage.tile([P, BATCH, PACK * PLACES], BF16, tag="stage", align_bytes=256)
-        nc.sync.dma_start(out=x_raw[:], in_=x.rearrange("n (p q) a b -> p n (q a b)", q=PACK))
+        ident = keep.tile([P, P], BF16)
+        make_identity(nc, ident[:])
+        nc.vector.tensor_copy(out=x_rows[:, 1, :], in_=x_rows[:, 0, :])
+        x_twice = x_rows[:].rearrange("p d r -> p (d r)")
         x_grouped = stage.tile([P, PLACES, BATCH, PACK], BF16, tag="stage", align_bytes=256)
-        x_by_place = x_raw[:].rearrange("p n (q s) -> p s n q", q=PACK)
-        for some in (slice(0, X_VECTOR // 2), slice(X_VECTOR // 2, X_VECTOR)):
-            nc.vector.tensor_copy(out=x_grouped[:, some, :, :], in_=x_by_place[:, some, :, :])
-        nc.scalar.copy(out=x_grouped[:, X_VECTOR:, :, :], in_=x_by_place[:, X_VECTOR:, :, :])
+        for s0 in range(0, PLACES, 2):
+            turned = psum.tile([P, 2, PACK, BATCH, 2], BF16, tag="acc")
+            for e in range(2):
+                for t in range(PACK):
+                    first = t * PLACES + s0 + e
+                    step = PACK * PLACES
+                    nc.tensor.transpose(
+                        turned[:, e, t, :, :].rearrange("p n f -> p (n f)"),
+                        x_twice[:, first : first + step * (P - 1) + 1 : step],
+                        ident[:],
+                    )
+            copy = nc.vector.tensor_copy if s0 % 4 == 0 else nc.scalar.copy
+            for f in range(2):
+                part = slice(f * half_p, (f + 1) * half_p)
+                copy(
+                    out=x_grouped[part, s0 : s0 + 2, :, :],
+                    in_=turned[part, :, :, :, f].rearrange("p s t n -> p s n t"),
+                )
         x_codes = keep.tile([P, PLACES + 1, BATCH], U32, align_bytes=64)
         x_scales = keep.tile([P, PLACES + 1, BATCH], U8, align_bytes=64)
         nc.gpsimd.memset(x_codes[:, PLACES, :].bitcast(I32), 0)
@@ -139,6 +157,8 @@ def tile_locallyconnected2d_kernel(tc, x, weight, bias, out):
                 scales=x_scales[:, some, :].rearrange("p s m -> p (s m)"),
                 in_=x_grouped[:, some, :, :].rearrange("p s n q -> p (s n q)"),
             )
+
+        lay_out(first_raw, 0, PIECE_O)
 
         bias_row = keep.tile([P, C_OUT * PLACES], BF16)
         nc.gpsimd.memset(bias_row[:], 0.0)

@@ -26,10 +26,12 @@ BANK = 512
 
 PIECE_O = 16
 SUB_O = 32
-SUBS = C_OUT // SUB_O
-LOADS = (PIECE_O, PIECE_O)
-LAST_LOADS = (PIECE_O, PIECE_O // 2, PIECE_O // 4, PIECE_O // 4)
-SUB_ROWS = SUB_O * PACK
+HALF_O = SUB_O // 2
+SUB_SIZES = (SUB_O,) * (C_OUT // SUB_O - 1) + (HALF_O, HALF_O)
+SUBS = len(SUB_SIZES)
+SUB_FIRST = [sum(SUB_SIZES[:k]) for k in range(SUBS)]
+WHOLE = (PIECE_O,)
+HALVES = (PIECE_O // 2, PIECE_O // 2)
 
 VALID_TAPS = 100
 FLOPS = 2 * BATCH * C_OUT * C_IN * VALID_TAPS
@@ -42,8 +44,9 @@ def valid_taps(place):
 N_GROUPS = 10
 GROUP_BLOCKS = 12
 BLOCKS = N_GROUPS * GROUP_BLOCKS
-PASS_BLOCKS = 4
-QUANTISE_BLOCKS = (8, 16, 32, 32, 16, 8, 8)
+PASS_O = 128
+ALIGN_O = 64
+QUANTISE_BLOCKS = (8, 32, 32, 32, 16)
 
 
 EMPTY_BLOCKS = (2, 9)
@@ -55,53 +58,89 @@ def block_of(w, j):
     return BLOCK_STEP * x_col + 1 - w
 
 
-LEFT = 2
-ROW_BLOCKS = SIDE + 4
-WINDOWS = ((0, 0, LEFT + 2), (3, 8, 0), (1, 2, LEFT), (2, 6, LEFT))
+def row_blocks(size):
+    return SIDE + 2 * (PASS_O // size - 2)
 
-ROWS = ((0,), (1, 2), (3,))
+
+def windows(size):
+    per_pass, align = PASS_O // size, ALIGN_O // size
+    result = []
+    for x_col in (0, SIDE - 1, 1, 2):
+        run = block_of(min(SIDE - 1, x_col + PAD), x_col + PAD - min(SIDE - 1, x_col + PAD))
+        first = GROUP_BLOCKS - per_pass if x_col == SIDE - 1 else run // align * align
+        result.append((x_col, first, per_pass - 2 + max(0, SIDE - 2 - x_col) - (run - first)))
+    return result
+
+
+ROWS = ((1, 2), (0,), (3,))
+BANK_ROWS = ((1, 2), (0, 3))
 VECTOR_PLACES = (((1, 2), 1), ((1, 2), 2), ((0,), 1))
-LAST_VECTOR_PLACES = VECTOR_PLACES + (((0,), 2), ((1, 2), 0))
+MORE_VECTOR_PLACES = VECTOR_PLACES + (((0,), 2), ((3,), 1), ((3,), 2))
 X_ROW = C_IN // 2 * PLACES
 
 
 def tile_locallyconnected2d_kernel(tc, x, weight, bias, out):
     nc = tc.nc
     places = [(rows, w) for rows in ROWS for w in range(SIDE)]
-    GROUPS = [(h, i) for h in range(SIDE) for i in range(*valid_taps(h))]
+    GROUPS = [(h, i) for rows in ROWS for h in rows for i in range(*valid_taps(h))]
     with ExitStack() as ctx:
         stage = ctx.enter_context(tc.tile_pool(name="stage", bufs=6))
         keep = ctx.enter_context(tc.tile_pool(name="keep", bufs=1))
-        work = ctx.enter_context(tc.tile_pool(name="work", bufs=2))
+        work = ctx.enter_context(tc.tile_pool(name="work", bufs=3))
         psum = ctx.enter_context(tc.psum_pool(name="psum", bufs=8))
-        ctx.enter_context(tc.manual_schedule(engines={mybir.EngineType.SP}))
+        ctx.enter_context(
+            tc.manual_schedule(engines={mybir.EngineType.SP, mybir.EngineType.DVE, mybir.EngineType.Activation})
+        )
 
         grouped = [
-            keep.tile([P, BLOCKS, SUB_ROWS], BF16, name="grouped_%d" % k, align_bytes=64) for k in range(2)
+            keep.tile([P, BLOCKS, SUB_O * PACK], BF16, name="grouped_%d" % k, align_bytes=64) for k in range(2)
         ]
-        for k in range(2):
-            for b in EMPTY_BLOCKS:
-                nc.vector.memset(
-                    grouped[k][:].rearrange("p (g b) r -> p g b r", b=GROUP_BLOCKS)[:, :, b, :].bitcast(I32), 0
-                )
         w_codes = keep.tile([P, BLOCKS, SUB_O], U32, align_bytes=64)
         w_scales = keep.tile([P, BLOCKS, SUB_O], U8, align_bytes=64)
 
         w_rows = weight.rearrange("u o (p q) h w t -> p (u o) (q h w t)", q=PACK)
         out_rows = out.rearrange("n o a b -> n o (a b)")
 
-        def load(o0, piece_o):
-            raw = stage.tile([P, piece_o, PACK * COLS], BF16, tag="stage", align_bytes=256)
-            nc.sync.dma_start(out=raw[:], in_=w_rows[:, o0 : o0 + piece_o, :])
-            return raw
+        def blocks_of(sub):
+            if SUB_SIZES[sub] == SUB_O:
+                return grouped[sub % 2][:]
+            halves = grouped[(SUBS - 4) % 2][:].rearrange("p b r -> p (b r)").rearrange("p (d b r) -> p d b r", d=2, b=BLOCKS)
+            return halves[:, sub - (SUBS - 2), :, :]
 
-        def lay_out(raw, o0, piece_o):
-            sub = o0 // SUB_O
-            by_group = grouped[sub % 2][:].rearrange("p (g b) r -> p g b r", b=GROUP_BLOCKS)
-            rows = raw[:].rearrange(
+        def codes_of(sub, tile):
+            if SUB_SIZES[sub] == SUB_O:
+                return tile[:]
+            halves = tile[:].rearrange("p b o -> p (b o)").rearrange("p (d b o) -> p d b o", d=2, b=BLOCKS)
+            return halves[:, sub - (SUBS - 2), :, :]
+
+        def clear(sub):
+            by_group = blocks_of(sub).rearrange("p (g b) r -> p g b r", b=GROUP_BLOCKS)
+            for b in EMPTY_BLOCKS:
+                nc.vector.memset(by_group[:, :, b, :].bitcast(I32), 0)
+
+        clear(0)
+        clear(1)
+
+        def load(o0, parts):
+            raw = stage.tile([P, PIECE_O, PACK * COLS], BF16, tag="stage", align_bytes=256)
+            result = []
+            first = 0
+            for piece_o in parts:
+                nc.sync.dma_start(
+                    out=raw[:, first : first + piece_o, :], in_=w_rows[:, o0 + first : o0 + first + piece_o, :]
+                )
+                result.append((raw, first, o0 + first, piece_o))
+                first += piece_o
+            return result
+
+        def lay_out(piece):
+            raw, first, o0, piece_o = piece
+            sub = max(k for k in range(SUBS) if SUB_FIRST[k] <= o0)
+            by_group = blocks_of(sub).rearrange("p (g b) r -> p g b r", b=GROUP_BLOCKS)
+            rows = raw[:, first : first + piece_o, :].rearrange(
                 "p o (q h w i j) -> p (o q) h w i j", q=PACK, h=SIDE, w=SIDE, i=KSIDE, j=KSIDE
             )
-            r0 = o0 % SUB_O * PACK
+            r0 = (o0 - SUB_FIRST[sub]) * PACK
             for tops, w in places:
                 i0, i1 = valid_taps(tops[0])
                 j0, j1 = valid_taps(w)
@@ -114,42 +153,60 @@ def tile_locallyconnected2d_kernel(tc, x, weight, bias, out):
                     b0 : b0 + BLOCK_STEP * (j1 - j0 - 1) + 1 : BLOCK_STEP,
                     r0 : r0 + piece_o * PACK,
                 ].rearrange("p (h i) j r -> p h i r j", h=len(tops))
-                if (tops, w) in (LAST_VECTOR_PLACES if sub == SUBS - 1 else VECTOR_PLACES):
+                if (tops, w) in (MORE_VECTOR_PLACES if sub == SUBS - 2 else VECTOR_PLACES):
                     nc.vector.tensor_copy(out=dst, in_=src)
                 else:
                     nc.scalar.copy(out=dst, in_=src)
 
-        half_p = P // 2
         x_rows = stage.tile([P, 2, X_ROW], BF16, tag="stage", align_bytes=256)
         nc.sync.dma_start(out=x_rows[:, 0, :], in_=x.rearrange("n (f c) a b -> (n f) (c a b)", f=2))
-        first_raw = load(0, PIECE_O)
+        first_pieces = load(0, WHOLE)
+        bias_row = keep.tile([P, C_OUT * PLACES], BF16)
+        nc.gpsimd.memset(bias_row[:], 0.0)
+        nc.sync.dma_start(out=bias_row[0:1, :], in_=bias.rearrange("u o a b -> u (o a b)"))
+        second_pieces = load(PIECE_O, WHOLE)
+
         ident = keep.tile([P, P], BF16)
         make_identity(nc, ident[:])
+        ones = keep.tile([P, P], BF16)
+        nc.vector.memset(ones[:], 1.0)
+        x_codes = keep.tile([P, PLACES + 1, BATCH], U32, align_bytes=64)
+        x_scales = keep.tile([P, PLACES + 1, BATCH], U8, align_bytes=64)
+        nc.gpsimd.memset(x_codes[:, PLACES, :].bitcast(I32), 0)
+        nc.gpsimd.memset(x_scales[:, PLACES, :].bitcast(I32), 0)
+
         nc.vector.tensor_copy(out=x_rows[:, 1, :], in_=x_rows[:, 0, :])
         x_twice = x_rows[:].rearrange("p d r -> p (d r)")
         x_grouped = stage.tile([P, PLACES, BATCH, PACK], BF16, tag="stage", align_bytes=256)
-        for s0 in range(0, PLACES, 2):
+
+        def turn_x(pair, engine_copy):
             turned = psum.tile([P, 2, PACK, BATCH, 2], BF16, tag="acc")
+            step = PACK * PLACES
             for e in range(2):
                 for t in range(PACK):
-                    first = t * PLACES + s0 + e
-                    step = PACK * PLACES
+                    first = t * PLACES + 2 * pair + e
                     nc.tensor.transpose(
                         turned[:, e, t, :, :].rearrange("p n f -> p (n f)"),
                         x_twice[:, first : first + step * (P - 1) + 1 : step],
                         ident[:],
                     )
-            copy = nc.vector.tensor_copy if s0 % 4 == 0 else nc.scalar.copy
             for f in range(2):
-                part = slice(f * half_p, (f + 1) * half_p)
-                copy(
-                    out=x_grouped[part, s0 : s0 + 2, :, :],
+                part = slice(f * (P // 2), (f + 1) * (P // 2))
+                engine_copy(
+                    out=x_grouped[part, 2 * pair : 2 * pair + 2, :, :],
                     in_=turned[part, :, :, :, f].rearrange("p s t n -> p s n t"),
                 )
-        x_codes = keep.tile([P, PLACES + 1, BATCH], U32, align_bytes=64)
-        x_scales = keep.tile([P, PLACES + 1, BATCH], U8, align_bytes=64)
-        nc.gpsimd.memset(x_codes[:, PLACES, :].bitcast(I32), 0)
-        nc.gpsimd.memset(x_scales[:, PLACES, :].bitcast(I32), 0)
+
+        turn_x(0, nc.vector.tensor_copy)
+        for piece in first_pieces:
+            lay_out(piece)
+        turn_x(1, nc.scalar.copy)
+        turn_x(2, nc.vector.tensor_copy)
+        turn_x(3, nc.scalar.copy)
+        for piece in second_pieces:
+            lay_out(piece)
+        for pair in range(4, PLACES // 2):
+            turn_x(pair, nc.scalar.copy if pair == 5 else nc.vector.tensor_copy)
         for lo in range(0, PLACES, PLACES // 2):
             some = slice(lo, lo + PLACES // 2)
             nc.vector.quantize_mx(
@@ -158,79 +215,121 @@ def tile_locallyconnected2d_kernel(tc, x, weight, bias, out):
                 in_=x_grouped[:, some, :, :].rearrange("p s n q -> p (s n q)"),
             )
 
-        lay_out(first_raw, 0, PIECE_O)
-
-        bias_row = keep.tile([P, C_OUT * PLACES], BF16)
-        nc.gpsimd.memset(bias_row[:], 0.0)
-        nc.sync.dma_start(out=bias_row[0:1, :], in_=bias.rearrange("u o a b -> u (o a b)"))
-        ones = keep.tile([P, P], BF16)
-        nc.vector.memset(ones[:], 1.0)
         bias_all = keep.tile([P, C_OUT, PLACES], BF16)
         bias_flat = bias_all[:].rearrange("p o s -> p (o s)")
-        for g in range(C_OUT * PLACES // (2 * BANK)):
-            spread = psum.tile([P, 2, BANK], BF16, tag="acc")
-            first = g * 2 * BANK
-            for k in range(2):
-                cols = slice(first + k * BANK, first + (k + 1) * BANK)
-                nc.tensor.matmul(out=spread[:, k, :], lhsT=ones[:], rhs=bias_row[:, cols], start=True, stop=True)
-            nc.vector.tensor_copy(
-                out=bias_flat[:, first : first + 2 * BANK], in_=spread[:].rearrange("p k n -> p (k n)")
-            )
 
-        results = []
-        for sub in range(SUBS):
-            o_first = sub * SUB_O
-            blocks = grouped[sub % 2]
-            o0 = o_first
-            for piece_o in LAST_LOADS if sub == SUBS - 1 else LOADS:
-                if o0 > 0:
-                    lay_out(load(o0, piece_o), o0, piece_o)
-                o0 += piece_o
+        def spread_bias():
+            for g in range(C_OUT * PLACES // (2 * BANK)):
+                spread = psum.tile([P, 2, BANK], BF16, tag="acc")
+                first = g * 2 * BANK
+                for k in range(2):
+                    cols = slice(first + k * BANK, first + (k + 1) * BANK)
+                    nc.tensor.matmul(out=spread[:, k, :], lhsT=ones[:], rhs=bias_row[:, cols], start=True, stop=True)
+                nc.vector.tensor_copy(
+                    out=bias_flat[:, first : first + 2 * BANK], in_=spread[:].rearrange("p k n -> p (k n)")
+                )
 
+        results = [
+            keep.tile([P, SUB_SIZES[sub], PLACES], F32, name="result_%d" % sub) for sub in range(SUBS)
+        ]
+        accs = {}
+
+        def quantise(sub):
             first = 0
             for n_blocks in QUANTISE_BLOCKS:
                 some = slice(first, first + n_blocks)
                 nc.vector.quantize_mx(
-                    out=w_codes[:, some, :].rearrange("p b o -> p (b o)").bitcast(FP8X4),
-                    scales=w_scales[:, some, :].rearrange("p b o -> p (b o)"),
-                    in_=blocks[:, some, :].rearrange("p b r -> p (b r)"),
+                    out=codes_of(sub, w_codes)[:, some, :].rearrange("p b o -> p (b o)").bitcast(FP8X4),
+                    scales=codes_of(sub, w_scales)[:, some, :].rearrange("p b o -> p (b o)"),
+                    in_=blocks_of(sub)[:, some, :].rearrange("p b r -> p (b r)"),
                 )
                 first += n_blocks
 
-            banks = []
-            for top in range(0, SIDE, 2):
-                acc = psum.tile([P, 2, ROW_BLOCKS, SUB_O], F32, tag="acc")
-                banks.append(acc)
-                for h in (top, top + 1):
-                    passes = [(i, window) for i in range(*valid_taps(h)) for window in WINDOWS]
+        def multiply(sub):
+            size = SUB_SIZES[sub]
+            per_pass = PASS_O // size
+            for k, bank_rows in enumerate(BANK_ROWS):
+                acc = psum.tile([P, 2, row_blocks(size), size], F32, tag="acc")
+                accs[(sub, k)] = acc
+                for r, h in enumerate(bank_rows):
+                    passes = [(i, window) for i in range(*valid_taps(h)) for window in windows(size)]
                     for i, window in passes:
                         x_col, first_block, first_out = window
                         x_place = (h + i - PAD) * SIDE + x_col
                         b = GROUPS.index((h, i)) * GROUP_BLOCKS + first_block
+                        moving = codes_of(sub, w_codes)[:, b : b + per_pass, :]
+                        moving_scales = codes_of(sub, w_scales)[:, b : b + per_pass, :]
                         nc.tensor.matmul_mx(
-                            out=acc[:, h - top, first_out : first_out + PASS_BLOCKS, :].rearrange("p b o -> p (b o)"),
+                            out=acc[:, r, first_out : first_out + per_pass, :].rearrange("p b o -> p (b o)"),
                             lhsT=x_codes[:, x_place : x_place + 2, :].rearrange("p s m -> p (s m)").bitcast(FP8X4),
                             lhsT_scale=x_scales[:, x_place : x_place + 2, :].rearrange("p s m -> p (s m)"),
-                            rhs=w_codes[:, b : b + PASS_BLOCKS, :].rearrange("p b o -> p (b o)").bitcast(FP8X4),
-                            rhs_scale=w_scales[:, b : b + PASS_BLOCKS, :].rearrange("p b o -> p (b o)"),
+                            rhs=moving.rearrange("p b o -> p (b o)").bitcast(FP8X4),
+                            rhs_scale=moving_scales.rearrange("p b o -> p (b o)"),
                             start=((i, window) == passes[0]),
                             stop=((i, window) == passes[-1]),
                         )
 
-            result = keep.tile([P, SUB_O, PLACES], F32, name="result_%d" % sub)
-            results.append(result)
+        sums = {}
+
+        def add_bias(sub):
+            size = SUB_SIZES[sub]
+            o0 = SUB_FIRST[sub]
+            left = PASS_O // size - 2
             biased = work.tile([P, SUB_O, PLACES], F32)
-            for k, acc in enumerate(banks):
-                some = slice(k * 2 * SIDE, (k + 1) * 2 * SIDE)
+            sums[sub] = biased
+            for k, (r0, r1) in enumerate(BANK_ROWS):
+                some = slice(r0, r1 + 1, r1 - r0)
                 nc.vector.tensor_tensor(
-                    out=biased[:, :, some].rearrange("p o (r w) -> p o r w", w=SIDE),
-                    in0=acc[:, :, LEFT : LEFT + SIDE, :].rearrange("p r w o -> p o r w")[:, :, :, ::-1],
-                    in1=bias_all[:, o_first : o_first + SUB_O, some].rearrange("p o (r w) -> p o r w", w=SIDE),
+                    out=biased[:, 0:size, :].rearrange("p o (h w) -> p o h w", w=SIDE)[:, :, some, :],
+                    in0=accs[(sub, k)][:, :, left : left + SIDE, :].rearrange("p r w o -> p o r w")[:, :, :, ::-1],
+                    in1=bias_all[:, o0 : o0 + size, :].rearrange("p o (h w) -> p o h w", w=SIDE)[:, :, some, :],
                     op=ALU.add,
                 )
+
+        def leaky(sub):
+            size = SUB_SIZES[sub]
             nc.vector.scalar_tensor_tensor(
-                out=result[:], in0=biased[:], scalar=NEG_SLOPE, in1=biased[:], op0=ALU.mult, op1=ALU.max
+                out=results[sub][:],
+                in0=sums[sub][:, 0:size, :],
+                scalar=NEG_SLOPE,
+                in1=sums[sub][:, 0:size, :],
+                op0=ALU.mult,
+                op1=ALU.max,
             )
 
+        for sub in range(SUBS - 2):
+            o0 = SUB_FIRST[sub]
+            if sub > 0:
+                for piece in load(o0, WHOLE):
+                    lay_out(piece)
+                if sub == 1:
+                    spread_bias()
+                add_bias(sub - 1)
+                leaky(sub - 1)
+                for piece in load(o0 + PIECE_O, HALVES if sub == SUBS - 3 else WHOLE):
+                    lay_out(piece)
+            quantise(sub)
+            multiply(sub)
+            if sub == SUBS - 4:
+                clear(SUBS - 2)
+                clear(SUBS - 1)
+
+        for piece in load(SUB_FIRST[SUBS - 2], HALVES):
+            lay_out(piece)
+        quantise(SUBS - 2)
+        multiply(SUBS - 2)
+        for k, piece in enumerate(load(SUB_FIRST[SUBS - 1], HALVES)):
+            lay_out(piece)
+            if k == 0:
+                add_bias(SUBS - 3)
+        quantise(SUBS - 1)
+        multiply(SUBS - 1)
+        leaky(SUBS - 3)
+        add_bias(SUBS - 2)
+        leaky(SUBS - 2)
+        add_bias(SUBS - 1)
+        leaky(SUBS - 1)
+
         for sub, result in enumerate(results):
-            nc.sync.dma_start(out=out_rows[:, sub * SUB_O : (sub + 1) * SUB_O, :], in_=result[0:BATCH, :, :])
+            o0 = SUB_FIRST[sub]
+            nc.sync.dma_start(out=out_rows[:, o0 : o0 + SUB_SIZES[sub], :], in_=result[0:BATCH, :, :])

@@ -46,7 +46,7 @@ GROUP_BLOCKS = 12
 BLOCKS = N_GROUPS * GROUP_BLOCKS
 PASS_O = 128
 ALIGN_O = 64
-QUANTISE_BLOCKS = (8, 32, 32, 32, 16)
+QUANTISE_BLOCKS = {SUB_O: (8, 32, 32, 32, 16), HALF_O: (16, 16, 16, 32, 32, 8)}
 
 
 EMPTY_BLOCKS = (2, 9)
@@ -74,14 +74,17 @@ def windows(size):
 
 ROWS = ((1, 2), (0,), (3,))
 BANK_ROWS = ((1, 2), (0, 3))
-VECTOR_PLACES = (((1, 2), 1), ((1, 2), 2), ((0,), 1))
-MORE_VECTOR_PLACES = VECTOR_PLACES + (((0,), 2), ((3,), 1), ((3,), 2))
+MIDDLE = (((1, 2), (1,)), ((1, 2), (2,)))
+SIDES = (((1, 2), (0,)), ((1, 2), (3,)))
+CORNERS = (((0,), (0, 3)), ((3,), (0, 3)))
+TOP_AND_BOTTOM = (((0,), (1, 2)), ((3,), (1, 2)))
+SHARES = (MIDDLE + (((0,), (1,)),), SIDES + CORNERS + (((0,), (2,)), TOP_AND_BOTTOM[1]))
+MORE_VECTOR = (MIDDLE + TOP_AND_BOTTOM, SIDES + CORNERS)
 X_ROW = C_IN // 2 * PLACES
 
 
 def tile_locallyconnected2d_kernel(tc, x, weight, bias, out):
     nc = tc.nc
-    places = [(rows, w) for rows in ROWS for w in range(SIDE)]
     GROUPS = [(h, i) for rows in ROWS for h in rows for i in range(*valid_taps(h))]
     with ExitStack() as ctx:
         stage = ctx.enter_context(tc.tile_pool(name="stage", bufs=6))
@@ -137,26 +140,36 @@ def tile_locallyconnected2d_kernel(tc, x, weight, bias, out):
             raw, first, o0, piece_o = piece
             sub = max(k for k in range(SUBS) if SUB_FIRST[k] <= o0)
             by_group = blocks_of(sub).rearrange("p (g b) r -> p g b r", b=GROUP_BLOCKS)
-            rows = raw[:, first : first + piece_o, :].rearrange(
-                "p o (q h w i j) -> p (o q) h w i j", q=PACK, h=SIDE, w=SIDE, i=KSIDE, j=KSIDE
-            )
             r0 = (o0 - SUB_FIRST[sub]) * PACK
-            for tops, w in places:
+            rows = raw[:, first : first + piece_o, :].rearrange("p o (q k) -> p (o q) k", q=PACK)
+            by_place = rows.rearrange("p r (h w i j) -> p r h w i j", h=SIDE, w=SIDE, i=KSIDE)
+
+            def views(tops, columns):
                 i0, i1 = valid_taps(tops[0])
-                j0, j1 = valid_taps(w)
                 g0 = GROUPS.index((tops[0], i0))
-                b0 = block_of(w, j0)
-                src = rows[:, :, tops[0] : tops[-1] + 1, w, i0:i1, j0:j1].rearrange("p r h i j -> p h i r j")
-                dst = by_group[
-                    :,
-                    g0 : g0 + len(tops) * (i1 - i0),
-                    b0 : b0 + BLOCK_STEP * (j1 - j0 - 1) + 1 : BLOCK_STEP,
-                    r0 : r0 + piece_o * PACK,
-                ].rearrange("p (h i) j r -> p h i r j", h=len(tops))
-                if (tops, w) in (MORE_VECTOR_PLACES if sub == SUBS - 2 else VECTOR_PLACES):
-                    nc.vector.tensor_copy(out=dst, in_=src)
-                else:
-                    nc.scalar.copy(out=dst, in_=src)
+                some = by_group[:, g0 : g0 + len(tops) * (i1 - i0), :, r0 : r0 + piece_o * PACK]
+                w = columns[0]
+                j0, j1 = valid_taps(w)
+                if len(columns) == 1:
+                    b0 = block_of(w, j0)
+                    src = by_place[:, :, tops[0] : tops[-1] + 1, w, i0:i1, j0:j1].rearrange("p r h i j -> p h i r j")
+                    dst = some[:, :, b0 : b0 + BLOCK_STEP * (j1 - j0 - 1) + 1 : BLOCK_STEP, :]
+                    return src, dst.rearrange("p (h i) j r -> p h i r j", h=len(tops))
+                if columns == (1, 2):
+                    src = by_place[:, :, tops[0], 1:3, i0:i1, :].rearrange("p r w i j -> p w i r j")
+                    dst = some.rearrange("p i (j b) r -> p i j b r", b=BLOCK_STEP)[:, :, :, 0:BLOCK_STEP:3, :]
+                    return src, dst.rearrange("p i j w r -> p w i r j")
+                start = (tops[0] * SIDE * KSIDE + i0) * KSIDE + j0
+                wide = rows[:, :, start - 4 : start + 35].rearrange("p r (x y) -> p r x y", y=13)
+                src = wide[:, :, 0:3:2, 4:10].rearrange("p r a (i j) -> p a i r j", j=KSIDE)[:, :, :, :, 0:2]
+                dst = some[:, :, 1:11, :].rearrange("p i (a b) r -> p a i b r", b=5)[:, :, :, 0:5:4, :]
+                return src, dst.rearrange("p a i j r -> p a i r j")
+
+            shares = MORE_VECTOR if sub == SUBS - 2 else SHARES
+            for engine_copy, share in zip((nc.vector.tensor_copy, nc.scalar.copy), shares):
+                for tops, columns in share:
+                    src, dst = views(tops, columns)
+                    engine_copy(out=dst, in_=src)
 
         x_rows = stage.tile([P, 2, X_ROW], BF16, tag="stage", align_bytes=256)
         nc.sync.dma_start(out=x_rows[:, 0, :], in_=x.rearrange("n (f c) a b -> (n f) (c a b)", f=2))
@@ -170,6 +183,8 @@ def tile_locallyconnected2d_kernel(tc, x, weight, bias, out):
         make_identity(nc, ident[:])
         ones = keep.tile([P, P], BF16)
         nc.vector.memset(ones[:], 1.0)
+        started = keep.tile([P, 1], BF16)
+        nc.scalar.copy(out=started[:], in_=ones[:, 0:1])
         x_codes = keep.tile([P, PLACES + 1, BATCH], U32, align_bytes=64)
         x_scales = keep.tile([P, PLACES + 1, BATCH], U8, align_bytes=64)
         nc.gpsimd.memset(x_codes[:, PLACES, :].bitcast(I32), 0)
@@ -206,7 +221,7 @@ def tile_locallyconnected2d_kernel(tc, x, weight, bias, out):
         for piece in second_pieces:
             lay_out(piece)
         for pair in range(4, PLACES // 2):
-            turn_x(pair, nc.scalar.copy if pair == 5 else nc.vector.tensor_copy)
+            turn_x(pair, nc.vector.tensor_copy)
         for lo in range(0, PLACES, PLACES // 2):
             some = slice(lo, lo + PLACES // 2)
             nc.vector.quantize_mx(
@@ -218,16 +233,20 @@ def tile_locallyconnected2d_kernel(tc, x, weight, bias, out):
         bias_all = keep.tile([P, C_OUT, PLACES], BF16)
         bias_flat = bias_all[:].rearrange("p o s -> p (o s)")
 
-        def spread_bias():
-            for g in range(C_OUT * PLACES // (2 * BANK)):
-                spread = psum.tile([P, 2, BANK], BF16, tag="acc")
-                first = g * 2 * BANK
-                for k in range(2):
-                    cols = slice(first + k * BANK, first + (k + 1) * BANK)
-                    nc.tensor.matmul(out=spread[:, k, :], lhsT=ones[:], rhs=bias_row[:, cols], start=True, stop=True)
-                nc.vector.tensor_copy(
-                    out=bias_flat[:, first : first + 2 * BANK], in_=spread[:].rearrange("p k n -> p (k n)")
+        spreads = []
+        for g in range(C_OUT * PLACES // (2 * BANK)):
+            spread = psum.tile([P, 2, BANK], BF16, tag="acc")
+            spreads.append(spread)
+            for k in range(2):
+                first = (2 * g + k) * BANK
+                nc.tensor.matmul(
+                    out=spread[:, k, :], lhsT=ones[:], rhs=bias_row[:, first : first + BANK], start=True, stop=True
                 )
+
+        def fetch_bias():
+            for g, spread in enumerate(spreads):
+                cols = slice(2 * g * BANK, 2 * (g + 1) * BANK)
+                nc.scalar.copy(out=bias_flat[:, cols], in_=spread[:].rearrange("p k n -> p (k n)"))
 
         results = [
             keep.tile([P, SUB_SIZES[sub], PLACES], F32, name="result_%d" % sub) for sub in range(SUBS)
@@ -236,7 +255,7 @@ def tile_locallyconnected2d_kernel(tc, x, weight, bias, out):
 
         def quantise(sub):
             first = 0
-            for n_blocks in QUANTISE_BLOCKS:
+            for n_blocks in QUANTISE_BLOCKS[SUB_SIZES[sub]]:
                 some = slice(first, first + n_blocks)
                 nc.vector.quantize_mx(
                     out=codes_of(sub, w_codes)[:, some, :].rearrange("p b o -> p (b o)").bitcast(FP8X4),
@@ -303,7 +322,7 @@ def tile_locallyconnected2d_kernel(tc, x, weight, bias, out):
                 for piece in load(o0, WHOLE):
                     lay_out(piece)
                 if sub == 1:
-                    spread_bias()
+                    fetch_bias()
                 add_bias(sub - 1)
                 leaky(sub - 1)
                 for piece in load(o0 + PIECE_O, HALVES if sub == SUBS - 3 else WHOLE):

from contextlib import ExitStack

import concourse.mybir as mybir
from concourse.masks import make_identity

FP8X4 = mybir.dt.float8_e4m3fn_x4
BF16 = mybir.dt.bfloat16
F32 = mybir.dt.float32
U32 = mybir.dt.uint32
U8 = mybir.dt.uint8
I32 = mybir.dt.int32
ALU = mybir.AluOpType

P = 128
PACK = 4
BATCH = 64
C_IN = P * PACK
C_OUT = 256
SIDE = 4
PLACES = SIDE * SIDE
KSIDE = 3
PAD = 1
COLS = PLACES * KSIDE * KSIDE
NEG_SLOPE = 0.1
BANK = 512

PIECE_O = 16
SUB_O = 32
HALF_O = SUB_O // 2
SUB_SIZES = (SUB_O,) * (C_OUT // SUB_O - 1) + (HALF_O, HALF_O)
SUBS = len(SUB_SIZES)
SUB_FIRST = [sum(SUB_SIZES[:k]) for k in range(SUBS)]
WHOLE = (PIECE_O,)
HALVES = (PIECE_O // 2, PIECE_O // 2)

VALID_TAPS = 100
FLOPS = 2 * BATCH * C_OUT * C_IN * VALID_TAPS


def valid_taps(place):
    return max(0, PAD - place), min(KSIDE, SIDE + PAD - place)


N_GROUPS = 10
GROUP_BLOCKS = 12
BLOCKS = N_GROUPS * GROUP_BLOCKS
PASS_O = 128
ALIGN_O = 64
QUANTISE_BLOCKS = {SUB_O: (8, 32, 32, 32, 16), HALF_O: (16, 16, 16, 32, 32, 8)}


EMPTY_BLOCKS = (2, 9)
BLOCK_STEP = SIDE


def block_of(w, j):
    x_col = w + j - PAD
    return BLOCK_STEP * x_col + 1 - w


def row_blocks(size):
    return SIDE + 2 * (PASS_O // size - 2)


def windows(size):
    per_pass, align = PASS_O // size, ALIGN_O // size
    result = []
    for x_col in (0, SIDE - 1, 1, 2):
        run = block_of(min(SIDE - 1, x_col + PAD), x_col + PAD - min(SIDE - 1, x_col + PAD))
        first = GROUP_BLOCKS - per_pass if x_col == SIDE - 1 else run // align * align
        result.append((x_col, first, per_pass - 2 + max(0, SIDE - 2 - x_col) - (run - first)))
    return result


ROWS = ((1, 2), (0,), (3,))
BANK_ROWS = ((1, 2), (0, 3))
MIDDLE = (((1, 2), (1,)), ((1, 2), (2,)))
SIDES = (((1, 2), (0,)), ((1, 2), (3,)))
CORNERS = (((0,), (0, 3)), ((3,), (0, 3)))
TOP_AND_BOTTOM = (((0,), (1, 2)), ((3,), (1, 2)))
SHARES = (MIDDLE + (((0,), (1,)),), SIDES + CORNERS + (((0,), (2,)), TOP_AND_BOTTOM[1]))
MORE_VECTOR = (MIDDLE + TOP_AND_BOTTOM, SIDES + CORNERS)
X_ROW = C_IN // 2 * PLACES


def tile_locallyconnected2d_kernel(tc, x, weight, bias, out):
    nc = tc.nc
    GROUPS = [(h, i) for rows in ROWS for h in rows for i in range(*valid_taps(h))]
    with ExitStack() as ctx:
        stage = ctx.enter_context(tc.tile_pool(name="stage", bufs=6))
        keep = ctx.enter_context(tc.tile_pool(name="keep", bufs=1))
        work = ctx.enter_context(tc.tile_pool(name="work", bufs=3))
        psum = ctx.enter_context(tc.psum_pool(name="psum", bufs=8))
        ctx.enter_context(
            tc.manual_schedule(engines={mybir.EngineType.SP, mybir.EngineType.DVE, mybir.EngineType.Activation})
        )

        grouped = [
            keep.tile([P, BLOCKS, SUB_O * PACK], BF16, name="grouped_%d" % k, align_bytes=64) for k in range(2)
        ]
        w_codes = keep.tile([P, BLOCKS, SUB_O], U32, align_bytes=64)
        w_scales = keep.tile([P, BLOCKS, SUB_O], U8, align_bytes=64)

        w_rows = weight.rearrange("u o (p q) h w t -> p (u o) (q h w t)", q=PACK)
        out_rows = out.rearrange("n o a b -> n o (a b)")

        def blocks_of(sub):
            if SUB_SIZES[sub] == SUB_O:
                return grouped[sub % 2][:]
            halves = grouped[(SUBS - 4) % 2][:].rearrange("p b r -> p (b r)").rearrange("p (d b r) -> p d b r", d=2, b=BLOCKS)
            return halves[:, sub - (SUBS - 2), :, :]

        def codes_of(sub, tile):
            if SUB_SIZES[sub] == SUB_O:
                return tile[:]
            halves = tile[:].rearrange("p b o -> p (b o)").rearrange("p (d b o) -> p d b o", d=2, b=BLOCKS)
            return halves[:, sub - (SUBS - 2), :, :]

        def clear(sub):
            by_group = blocks_of(sub).rearrange("p (g b) r -> p g b r", b=GROUP_BLOCKS)
            for b in EMPTY_BLOCKS:
                nc.vector.memset(by_group[:, :, b, :].bitcast(I32), 0)

        clear(0)
        clear(1)

        def load(o0, parts):
            raw = stage.tile([P, PIECE_O, PACK * COLS], BF16, tag="stage", align_bytes=256)
            result = []
            first = 0
            for piece_o in parts:
                nc.sync.dma_start(
                    out=raw[:, first : first + piece_o, :], in_=w_rows[:, o0 + first : o0 + first + piece_o, :]
                )
                result.append((raw, first, o0 + first, piece_o))
                first += piece_o
            return result

        def lay_out(piece):
            raw, first, o0, piece_o = piece
            sub = max(k for k in range(SUBS) if SUB_FIRST[k] <= o0)
            by_group = blocks_of(sub).rearrange("p (g b) r -> p g b r", b=GROUP_BLOCKS)
            r0 = (o0 - SUB_FIRST[sub]) * PACK
            rows = raw[:, first : first + piece_o, :].rearrange("p o (q k) -> p (o q) k", q=PACK)
            by_place = rows.rearrange("p r (h w i j) -> p r h w i j", h=SIDE, w=SIDE, i=KSIDE)

            def views(tops, columns):
                i0, i1 = valid_taps(tops[0])
                g0 = GROUPS.index((tops[0], i0))
                some = by_group[:, g0 : g0 + len(tops) * (i1 - i0), :, r0 : r0 + piece_o * PACK]
                w = columns[0]
                j0, j1 = valid_taps(w)
                if len(columns) == 1:
                    b0 = block_of(w, j0)
                    src = by_place[:, :, tops[0] : tops[-1] + 1, w, i0:i1, j0:j1].rearrange("p r h i j -> p h i r j")
                    dst = some[:, :, b0 : b0 + BLOCK_STEP * (j1 - j0 - 1) + 1 : BLOCK_STEP, :]
                    return src, dst.rearrange("p (h i) j r -> p h i r j", h=len(tops))
                if columns == (1, 2):
                    src = by_place[:, :, tops[0], 1:3, i0:i1, :].rearrange("p r w i j -> p w i r j")
                    dst = some.rearrange("p i (j b) r -> p i j b r", b=BLOCK_STEP)[:, :, :, 0:BLOCK_STEP:3, :]
                    return src, dst.rearrange("p i j w r -> p w i r j")
                start = (tops[0] * SIDE * KSIDE + i0) * KSIDE + j0
                wide = rows[:, :, start - 4 : start + 35].rearrange("p r (x y) -> p r x y", y=13)
                src = wide[:, :, 0:3:2, 4:10].rearrange("p r a (i j) -> p a i r j", j=KSIDE)[:, :, :, :, 0:2]
                dst = some[:, :, 1:11, :].rearrange("p i (a b) r -> p a i b r", b=5)[:, :, :, 0:5:4, :]
                return src, dst.rearrange("p a i j r -> p a i r j")

            shares = MORE_VECTOR if sub == SUBS - 2 else SHARES
            for engine_copy, share in zip((nc.vector.tensor_copy, nc.scalar.copy), shares):
                for tops, columns in share:
                    src, dst = views(tops, columns)
                    engine_copy(out=dst, in_=src)

        x_rows = stage.tile([P, 2, X_ROW], BF16, tag="stage", align_bytes=256)
        nc.sync.dma_start(out=x_rows[:, 0, :], in_=x.rearrange("n (f c) a b -> (n f) (c a b)", f=2))
        first_pieces = load(0, WHOLE)
        bias_row = keep.tile([P, C_OUT * PLACES], BF16)
        nc.gpsimd.memset(bias_row[:], 0.0)
        nc.sync.dma_start(out=bias_row[0:1, :], in_=bias.rearrange("u o a b -> u (o a b)"))
        second_pieces = load(PIECE_O, WHOLE)

        ident = keep.tile([P, P], BF16)
        make_identity(nc, ident[:])
        ones = keep.tile([P, P], BF16)
        nc.vector.memset(ones[:], 1.0)
        started = keep.tile([P, 1], BF16)
        nc.scalar.copy(out=started[:], in_=ones[:, 0:1])
        x_codes = keep.tile([P, PLACES + 1, BATCH], U32, align_bytes=64)
        x_scales = keep.tile([P, PLACES + 1, BATCH], U8, align_bytes=64)
        nc.gpsimd.memset(x_codes[:, PLACES, :].bitcast(I32), 0)
        nc.gpsimd.memset(x_scales[:, PLACES, :].bitcast(I32), 0)

        nc.vector.tensor_copy(out=x_rows[:, 1, :], in_=x_rows[:, 0, :])
        x_twice = x_rows[:].rearrange("p d r -> p (d r)")
        x_grouped = stage.tile([P, PLACES, BATCH, PACK], BF16, tag="stage", align_bytes=256)

        def turn_x(pair, engine_copy):
            turned = psum.tile([P, 2, PACK, BATCH, 2], BF16, tag="acc")
            step = PACK * PLACES
            for e in range(2):
                for t in range(PACK):
                    first = t * PLACES + 2 * pair + e
                    nc.tensor.transpose(
                        turned[:, e, t, :, :].rearrange("p n f -> p (n f)"),
                        x_twice[:, first : first + step * (P - 1) + 1 : step],
                        ident[:],
                    )
            for f in range(2):
                part = slice(f * (P // 2), (f + 1) * (P // 2))
                engine_copy(
                    out=x_grouped[part, 2 * pair : 2 * pair + 2, :, :],
                    in_=turned[part, :, :, :, f].rearrange("p s t n -> p s n t"),
                )

        turn_x(0, nc.vector.tensor_copy)
        for piece in first_pieces:
            lay_out(piece)
        turn_x(1, nc.scalar.copy)
        turn_x(2, nc.vector.tensor_copy)
        turn_x(3, nc.scalar.copy)
        for piece in second_pieces:
            lay_out(piece)
        for pair in range(4, PLACES // 2):
            turn_x(pair, nc.vector.tensor_copy)
        for lo in range(0, PLACES, PLACES // 2):
            some = slice(lo, lo + PLACES // 2)
            nc.vector.quantize_mx(
                out=x_codes[:, some, :].rearrange("p s m -> p (s m)").bitcast(FP8X4),
                scales=x_scales[:, some, :].rearrange("p s m -> p (s m)"),
                in_=x_grouped[:, some, :, :].rearrange("p s n q -> p (s n q)"),
            )

        bias_all = keep.tile([P, C_OUT, PLACES], BF16)
        bias_flat = bias_all[:].rearrange("p o s -> p (o s)")

        spreads = []
        for g in range(C_OUT * PLACES // (2 * BANK)):
            spread = psum.tile([P, 2, BANK], BF16, tag="acc")
            spreads.append(spread)
            for k in range(2):
                first = (2 * g + k) * BANK
                nc.tensor.matmul(
                    out=spread[:, k, :], lhsT=ones[:], rhs=bias_row[:, first : first + BANK], start=True, stop=True
                )

        def fetch_bias():
            for g, spread in enumerate(spreads):
                cols = slice(2 * g * BANK, 2 * (g + 1) * BANK)
                nc.scalar.copy(out=bias_flat[:, cols], in_=spread[:].rearrange("p k n -> p (k n)"))

        results = [
            keep.tile([P, SUB_SIZES[sub], PLACES], F32, name="result_%d" % sub) for sub in range(SUBS)
        ]
        accs = {}

        def quantise(sub):
            first = 0
            for n_blocks in QUANTISE_BLOCKS[SUB_SIZES[sub]]:
                some = slice(first, first + n_blocks)
                nc.vector.quantize_mx(
                    out=codes_of(sub, w_codes)[:, some, :].rearrange("p b o -> p (b o)").bitcast(FP8X4),
                    scales=codes_of(sub, w_scales)[:, some, :].rearrange("p b o -> p (b o)"),
                    in_=blocks_of(sub)[:, some, :].rearrange("p b r -> p (b r)"),
                )
                first += n_blocks

        def multiply(sub):
            size = SUB_SIZES[sub]
            per_pass = PASS_O // size
            for k, bank_rows in enumerate(BANK_ROWS):
                acc = psum.tile([P, 2, row_blocks(size), size], F32, tag="acc")
                accs[(sub, k)] = acc
                for r, h in enumerate(bank_rows):
                    passes = [(i, window) for i in range(*valid_taps(h)) for window in windows(size)]
                    for i, window in passes:
                        x_col, first_block, first_out = window
                        x_place = (h + i - PAD) * SIDE + x_col
                        b = GROUPS.index((h, i)) * GROUP_BLOCKS + first_block
                        moving = codes_of(sub, w_codes)[:, b : b + per_pass, :]
                        moving_scales = codes_of(sub, w_scales)[:, b : b + per_pass, :]
                        nc.tensor.matmul_mx(
                            out=acc[:, r, first_out : first_out + per_pass, :].rearrange("p b o -> p (b o)"),
                            lhsT=x_codes[:, x_place : x_place + 2, :].rearrange("p s m -> p (s m)").bitcast(FP8X4),
                            lhsT_scale=x_scales[:, x_place : x_place + 2, :].rearrange("p s m -> p (s m)"),
                            rhs=moving.rearrange("p b o -> p (b o)").bitcast(FP8X4),
                            rhs_scale=moving_scales.rearrange("p b o -> p (b o)"),
                            start=((i, window) == passes[0]),
                            stop=((i, window) == passes[-1]),
                        )

        sums = {}

        def add_bias(sub):
            size = SUB_SIZES[sub]
            o0 = SUB_FIRST[sub]
            left = PASS_O // size - 2
            biased = work.tile([P, SUB_O, PLACES], F32)
            sums[sub] = biased
            for k, (r0, r1) in enumerate(BANK_ROWS):
                some = slice(r0, r1 + 1, r1 - r0)
                nc.vector.tensor_tensor(
                    out=biased[:, 0:size, :].rearrange("p o (h w) -> p o h w", w=SIDE)[:, :, some, :],
                    in0=accs[(sub, k)][:, :, left : left + SIDE, :].rearrange("p r w o -> p o r w")[:, :, :, ::-1],
                    in1=bias_all[:, o0 : o0 + size, :].rearrange("p o (h w) -> p o h w", w=SIDE)[:, :, some, :],
                    op=ALU.add,
                )

        def leaky(sub):
            size = SUB_SIZES[sub]
            nc.vector.scalar_tensor_tensor(
                out=results[sub][:],
                in0=sums[sub][:, 0:size, :],
                scalar=NEG_SLOPE,
                in1=sums[sub][:, 0:size, :],
                op0=ALU.mult,
                op1=ALU.max,
            )

        for sub in range(SUBS - 2):
            o0 = SUB_FIRST[sub]
            if sub > 0:
                for piece in load(o0, WHOLE):
                    lay_out(piece)
                if sub == 1:
                    fetch_bias()
                add_bias(sub - 1)
                leaky(sub - 1)
                for piece in load(o0 + PIECE_O, HALVES if sub == SUBS - 3 else WHOLE):
                    lay_out(piece)
            quantise(sub)
            multiply(sub)
            if sub == SUBS - 4:
                clear(SUBS - 2)
                clear(SUBS - 1)

        for piece in load(SUB_FIRST[SUBS - 2], HALVES):
            lay_out(piece)
        quantise(SUBS - 2)
        multiply(SUBS - 2)
        for k, piece in enumerate(load(SUB_FIRST[SUBS - 1], HALVES)):
            lay_out(piece)
            if k == 0:
                add_bias(SUBS - 3)
        quantise(SUBS - 1)
        multiply(SUBS - 1)
        leaky(SUBS - 3)
        add_bias(SUBS - 2)
        leaky(SUBS - 2)
        add_bias(SUBS - 1)
        leaky(SUBS - 1)

        for sub, result in enumerate(results):
            o0 = SUB_FIRST[sub]
            nc.sync.dma_start(out=out_rows[:, o0 : o0 + SUB_SIZES[sub], :], in_=result[0:BATCH, :, :])
